import numpy as np
import ml_dtypes


def mxq(x, axis, fmt="e4m3"):
    dtype, down = {"e4m3": (ml_dtypes.float8_e4m3fn, 7), "e5m2": (ml_dtypes.float8_e5m2, 14)}[fmt]
    v = np.moveaxis(np.asarray(x, np.float32).astype(ml_dtypes.bfloat16).astype(np.float64), axis, -1)
    blocks = v.reshape(v.shape[:-1] + (-1, 32))
    amax = np.abs(blocks).max(-1, keepdims=True)
    byte = np.maximum(np.where(amax > 0, np.frexp(amax)[1] - 1 + 127, 0) - down, 1)
    scale = np.exp2(byte - 127.0)
    codes = (blocks / scale).astype(np.float32).astype(dtype).astype(np.float64)
    return np.moveaxis((codes * scale).reshape(v.shape), -1, axis)


WIDE = False


def mx_kscale(k):
    if not WIDE:
        return np.ones(k)
    levels = np.array([10, -10, 5, -5, 0])
    a = np.random.permutation(np.resize(levels, k // 512 * 4)).reshape(k // 512, 4)
    idx = np.arange(k)
    return np.exp2(a[idx // 512, idx % 128 // 32])


BF16 = ml_dtypes.bfloat16


def bf(x):
    return np.asarray(x, np.float32).astype(BF16)


def f64(x):
    return np.asarray(x).astype(np.float64)


B, N, F, T, DE, FO, K = 2, 1024, 16, 16, 16, 32, 3
C = F * T


def setup_inputs():
    s = mx_kscale(N)
    return {"supports": bf(np.abs(np.random.standard_normal((N, N))) * 0.4 / np.sqrt(N)),
            "cheb_2": bf(np.random.standard_normal((N, N)) * 0.8 / np.sqrt(N)),
            "spatial_attention": bf(np.random.random((B, N, N)) * s[None, :, None]),
            "x": bf(np.random.standard_normal((B, N, F, T)) / s[None, :, None, None])}


def reference(supports, cheb_2, spatial_attention, x):
    at = f64(spatial_attention)
    xs = f64(x).reshape(B, N, C)
    xq = mxq(xs, 1, "e4m3")
    r0 = np.diagonal(at, axis1=1, axis2=2)[:, :, None] * xs
    r1 = mxq(f64(supports)[None] * at, 1, "e4m3").transpose(0, 2, 1) @ xq
    r2 = mxq(f64(cheb_2)[None] * at, 1, "e4m3").transpose(0, 2, 1) @ xq
    return np.stack([r0, r1, r2]).reshape(K, B, N, F, T)

@@ -1,0 +1,221 @@
+from contextlib import ExitStack
+
+import concourse.mybir as mybir
+
+BF16 = mybir.dt.bfloat16
+F32 = mybir.dt.float32
+U32 = mybir.dt.uint32
+U8 = mybir.dt.uint8
+FP8X4 = mybir.dt.float8_e4m3fn_x4
+
+P = 128
+PACK = 4
+SAMPLES = 2
+TERMS = 2
+NODES = 1024
+SIGNAL = 256
+PASSES = NODES // (P * PACK)
+UNIT = 512
+UNITS = NODES // UNIT
+M_TILE = 128
+BANK_TILES = 2
+RUN = 4
+BLOCK = 16
+VECTOR_COLS = (128, 256)
+
+FLOPS = 2 * TERMS * SAMPLES * NODES * NODES * SIGNAL
+
+
+def regroup(engine_copy, grouped, rows):
+    engine_copy(
+        out=grouped.rearrange("p (g i) j -> p g j i", i=RUN),
+        in_=rows.rearrange("p j (g i) -> p g j i", i=RUN),
+    )
+
+
+def tile_napl_conv_withsat_pb_kernel(tc, supports, cheb_2, spatial_attention, x, out):
+    nc = tc.nc
+    terms = (supports, cheb_2)
+    with ExitStack() as ctx:
+        keep = ctx.enter_context(tc.tile_pool(name="keep", bufs=1))
+        stage = ctx.enter_context(tc.tile_pool(name="stage", bufs=3))
+        psum = ctx.enter_context(tc.psum_pool(name="psum", bufs=8))
+        ctx.enter_context(tc.manual_schedule())
+
+        term_sb = {}
+        att_sb = {}
+        codes = {}
+        scales = {}
+        for c in range(PASSES):
+            for k in range(TERMS):
+                term_sb[k, c] = keep.tile([P, PACK, NODES], BF16, name="term%d_%d" % (k, c))
+            for b in range(SAMPLES):
+                att_sb[b, c] = keep.tile([P, PACK, NODES], BF16, name="att%d_%d" % (b, c))
+        for b in range(SAMPLES):
+            for k in range(TERMS):
+                codes[b, k] = keep.tile(
+                    [P, PASSES, NODES], U32, name="codes%d_%d" % (b, k), align_bytes=64
+                )
+                scales[b, k] = keep.tile(
+                    [P, PASSES, NODES], U8, name="scales%d_%d" % (b, k), align_bytes=64
+                )
+        x_sb = keep.tile([P, SAMPLES, PASSES, PACK, SIGNAL], BF16)
+        x_grouped = keep.tile([P, SAMPLES, PASSES, SIGNAL, PACK], BF16, align_bytes=64)
+        x_codes = keep.tile([P, SAMPLES, PASSES, SIGNAL], U32, align_bytes=64)
+        x_scales = keep.tile([P, SAMPLES, PASSES, SIGNAL], U8, align_bytes=64)
+        diag_bf = keep.tile([P, SAMPLES, PASSES, BLOCK], BF16)
+        diag = keep.tile([P, SAMPLES, PASSES, PACK], F32)
+
+        def load_signal(b):
+            nc.sync.dma_start(
+                out=x_sb[:, b].rearrange("p c j s -> p c (j s)"),
+                in_=x[b].rearrange("(c p j) f t -> p c (j f t)", p=P, j=PACK),
+            )
+
+        def load_diagonal(b):
+            flat = spatial_attention[b].rearrange("n m -> (n m)")
+            on_diagonal = flat[0 : NODES * NODES : NODES + 1]
+            with nc.allow_non_contiguous_dma(reason="a diagonal has no two neighbours"):
+                for c in range(PASSES):
+                    nc.sync.dma_start(
+                        out=diag_bf[:, b, c, :PACK],
+                        in_=on_diagonal.rearrange("(c p j) -> c p j", p=P, j=PACK)[c],
+                    )
+
+        def load_columns(slab, matrix, c, cols):
+            rows = matrix[c * P * PACK : (c + 1) * P * PACK, :]
+            nc.sync.dma_start(
+                out=slab[:, :, cols], in_=rows.rearrange("(p j) m -> p j m", j=PACK)[:, :, cols]
+            )
+
+        unit_cols = [slice(u * UNIT, (u + 1) * UNIT) for u in range(UNITS)]
+        whole = slice(0, NODES)
+        load_signal(0)
+        load_columns(term_sb[0, 0], terms[0], 0, unit_cols[0])
+        load_columns(att_sb[0, 0], spatial_attention[0], 0, unit_cols[0])
+        load_diagonal(0)
+        load_columns(term_sb[1, 0], terms[1], 0, unit_cols[0])
+        load_columns(term_sb[0, 0], terms[0], 0, unit_cols[1])
+        load_columns(att_sb[0, 0], spatial_attention[0], 0, unit_cols[1])
+        load_columns(term_sb[1, 0], terms[1], 0, unit_cols[1])
+        load_signal(1)
+        load_diagonal(1)
+        load_columns(att_sb[1, 0], spatial_attention[1], 0, unit_cols[0])
+        load_columns(att_sb[1, 0], spatial_attention[1], 0, unit_cols[1])
+        load_columns(term_sb[0, 1], terms[0], 1, whole)
+        load_columns(att_sb[0, 1], spatial_attention[0], 1, whole)
+        load_columns(term_sb[1, 1], terms[1], 1, whole)
+        load_columns(att_sb[1, 1], spatial_attention[1], 1, whole)
+
+        def quantise_signal(b):
+            for c in range(PASSES):
+                regroup(nc.vector.tensor_copy, x_grouped[:, b, c], x_sb[:, b, c])
+            nc.vector.quantize_mx(
+                out=x_codes[:, b].rearrange("p c s -> p (c s)").bitcast(FP8X4),
+                scales=x_scales[:, b].rearrange("p c s -> p (c s)"),
+                in_=x_grouped[:, b].rearrange("p c s j -> p (c s j)"),
+            )
+
+        def widen_diagonal(b):
+            nc.scalar.copy(out=diag[:, b], in_=diag_bf[:, b, :, :PACK])
+
+        def scale_rows(b, c, half):
+            scaled = keep.tile([P, PACK // 2, SIGNAL], F32, name="scaled%d_%d_%d" % (b, c, half))
+            for i in range(PACK // 2):
+                j = half * (PACK // 2) + i
+                nc.scalar.activation(
+                    out=scaled[:, i, :],
+                    in_=x_sb[:, b, c, j, :],
+                    func=mybir.ActivationFunctionType.Copy,
+                    scale=diag[:, b, c, j : j + 1],
+                )
+            rows = out[0, b].rearrange("(c p h i) f t -> c h p (i f t)", p=P, h=2, i=PACK // 2)
+            nc.sync.dma_start(out=rows[c, half], in_=scaled[:].rearrange("p i s -> p (i s)"))
+
+        def multiply(c, b, k, u):
+            cols = slice(u * UNIT, (u + 1) * UNIT)
+            product = stage.tile([P, PACK, UNIT], BF16)
+            nc.vector.tensor_tensor(
+                out=product[:],
+                in0=term_sb[k, c][:, :, cols],
+                in1=att_sb[b, c][:, :, cols],
+                op=mybir.AluOpType.mult,
+            )
+            return product
+
+        def regroup_product(c, product):
+            split = VECTOR_COLS[c]
+            grouped = stage.tile([P, UNIT, PACK], BF16, align_bytes=64)
+            regroup(nc.vector.tensor_copy, grouped[:, :split, :], product[:, :, :split])
+            regroup(nc.scalar.copy, grouped[:, split:, :], product[:, :, split:])
+            return grouped
+
+        def quantise(c, b, k, u, grouped):
+            cols = slice(u * UNIT, (u + 1) * UNIT)
+            nc.vector.quantize_mx(
+                out=codes[b, k][:, c, cols].bitcast(FP8X4),
+                scales=scales[b, k][:, c, cols],
+                in_=grouped[:].rearrange("p w j -> p (w j)"),
+            )
+
+        def contract(b, k, u):
+            banks = []
+            for bank in range(UNIT // (BANK_TILES * M_TILE)):
+                acc = psum.tile([P, BANK_TILES, SIGNAL], F32)
+                for i in range(BANK_TILES):
+                    first = u * UNIT + (bank * BANK_TILES + i) * M_TILE
+                    m_cols = slice(first, first + M_TILE)
+                    for c in range(PASSES):
+                        nc.tensor.matmul_mx(
+                            out=acc[:, i, :],
+                            lhsT=codes[b, k][:, c, m_cols].bitcast(FP8X4),
+                            lhsT_scale=scales[b, k][:, c, m_cols],
+                            rhs=x_codes[:, b, c, :].bitcast(FP8X4),
+                            rhs_scale=x_scales[:, b, c, :],
+                            start=(c == 0),
+                            stop=(c == PASSES - 1),
+                        )
+                banks.append(acc)
+            return banks
+
+        def empty_and_store(b, k, u, banks):
+            result = keep.tile(
+                [P, UNIT // M_TILE, SIGNAL], F32, name="result%d_%d_%d" % (b, k, u)
+            )
+            for bank, acc in enumerate(banks):
+                nc.scalar.copy(
+                    out=result[:, bank * BANK_TILES : (bank + 1) * BANK_TILES, :], in_=acc[:]
+                )
+            rows = out[1 + k, b].rearrange("(u t p) f s -> u p t (f s)", t=UNIT // M_TILE, p=P)
+            nc.sync.dma_start(out=rows[u], in_=result[:])
+
+        rounds = []
+        for c in range(PASSES):
+            for b in range(SAMPLES):
+                for u in range(UNITS):
+                    for k in range(TERMS):
+                        rounds.append((c, b, k, u))
+
+        products = {}
+        groupeds = {}
+        sums = {}
+        for s in range(-1, len(rounds) + 2):
+            if 0 <= s < len(rounds):
+                c, b, k, u = rounds[s]
+                if c == 0:
+                    scale_rows(b, k, u)
+                groupeds[s] = regroup_product(c, products[s])
+            if s + 1 < len(rounds):
+                c, b, k, u = rounds[s + 1]
+                if (c, k, u) == (0, 0, 0):
+                    quantise_signal(b)
+                    widen_diagonal(b)
+                products[s + 1] = multiply(c, b, k, u)
+            if 0 <= s - 1 < len(rounds):
+                c, b, k, u = rounds[s - 1]
+                quantise(c, b, k, u, groupeds[s - 1])
+                if c == PASSES - 1:
+                    sums[s - 1] = contract(b, k, u)
+            if s - 2 in sums:
+                c, b, k, u = rounds[s - 2]
+                empty_and_store(b, k, u, sums[s - 2])

@@ -15,13 +15,16 @@ TERMS = 2
 NODES = 1024
 SIGNAL = 256
 PASSES = NODES // (P * PACK)
+LAST = PASSES - 1
 UNIT = 512
 UNITS = NODES // UNIT
 M_TILE = 128
 BANK_TILES = 2
+BANK_COLS = BANK_TILES * M_TILE
+BANKS = UNIT // BANK_COLS
 RUN = 4
 BLOCK = 16
-VECTOR_COLS = (128, 256)
+VECTOR_COLS = (96, 256)
 
 FLOPS = 2 * TERMS * SAMPLES * NODES * NODES * SIGNAL
 
@@ -66,13 +69,23 @@ def tile_napl_conv_withsat_pb_kernel(tc, supports, cheb_2, spatial_attention, x,
         diag_bf = keep.tile([P, SAMPLES, PASSES, BLOCK], BF16)
         diag = keep.tile([P, SAMPLES, PASSES, PACK], F32)
 
-        def load_signal(b):
+        def load_columns(slab, matrix, c, cols):
+            rows = matrix[c * P * PACK : (c + 1) * P * PACK, :]
+            nc.sync.dma_start(
+                out=slab[:, :, cols], in_=rows.rearrange("(p j) m -> p j m", j=PACK)[:, :, cols]
+            )
+
+        def load_matrices(c, cols):
+            load_columns(term_sb[0, c], terms[0], c, cols)
+            load_columns(att_sb[0, c], spatial_attention[0], c, cols)
+            load_columns(term_sb[1, c], terms[1], c, cols)
+            load_columns(att_sb[1, c], spatial_attention[1], c, cols)
+
+        for b in range(SAMPLES):
             nc.sync.dma_start(
                 out=x_sb[:, b].rearrange("p c j s -> p c (j s)"),
                 in_=x[b].rearrange("(c p j) f t -> p c (j f t)", p=P, j=PACK),
             )
-
-        def load_diagonal(b):
             flat = spatial_attention[b].rearrange("n m -> (n m)")
             on_diagonal = flat[0 : NODES * NODES : NODES + 1]
             with nc.allow_non_contiguous_dma(reason="a diagonal has no two neighbours"):
@@ -81,33 +94,11 @@ def tile_napl_conv_withsat_pb_kernel(tc, supports, cheb_2, spatial_attention, x,
                         out=diag_bf[:, b, c, :PACK],
                         in_=on_diagonal.rearrange("(c p j) -> c p j", p=P, j=PACK)[c],
                     )
+        for u in range(UNITS):
+            load_matrices(0, slice(u * UNIT, (u + 1) * UNIT))
+        load_matrices(LAST, slice(0, NODES))
 
-        def load_columns(slab, matrix, c, cols):
-            rows = matrix[c * P * PACK : (c + 1) * P * PACK, :]
-            nc.sync.dma_start(
-                out=slab[:, :, cols], in_=rows.rearrange("(p j) m -> p j m", j=PACK)[:, :, cols]
-            )
-
-        unit_cols = [slice(u * UNIT, (u + 1) * UNIT) for u in range(UNITS)]
-        whole = slice(0, NODES)
-        load_signal(0)
-        load_columns(term_sb[0, 0], terms[0], 0, unit_cols[0])
-        load_columns(att_sb[0, 0], spatial_attention[0], 0, unit_cols[0])
-        load_diagonal(0)
-        load_columns(term_sb[1, 0], terms[1], 0, unit_cols[0])
-        load_columns(term_sb[0, 0], terms[0], 0, unit_cols[1])
-        load_columns(att_sb[0, 0], spatial_attention[0], 0, unit_cols[1])
-        load_columns(term_sb[1, 0], terms[1], 0, unit_cols[1])
-        load_signal(1)
-        load_diagonal(1)
-        load_columns(att_sb[1, 0], spatial_attention[1], 0, unit_cols[0])
-        load_columns(att_sb[1, 0], spatial_attention[1], 0, unit_cols[1])
-        load_columns(term_sb[0, 1], terms[0], 1, whole)
-        load_columns(att_sb[0, 1], spatial_attention[0], 1, whole)
-        load_columns(term_sb[1, 1], terms[1], 1, whole)
-        load_columns(att_sb[1, 1], spatial_attention[1], 1, whole)
-
-        def quantise_signal(b):
+        for b in range(SAMPLES):
             for c in range(PASSES):
                 regroup(nc.vector.tensor_copy, x_grouped[:, b, c], x_sb[:, b, c])
             nc.vector.quantize_mx(
@@ -116,21 +107,20 @@ def tile_napl_conv_withsat_pb_kernel(tc, supports, cheb_2, spatial_attention, x,
                 in_=x_grouped[:, b].rearrange("p c s j -> p (c s j)"),
             )
 
-        def widen_diagonal(b):
             nc.scalar.copy(out=diag[:, b], in_=diag_bf[:, b, :, :PACK])
-
-        def scale_rows(b, c, half):
-            scaled = keep.tile([P, PACK // 2, SIGNAL], F32, name="scaled%d_%d_%d" % (b, c, half))
-            for i in range(PACK // 2):
-                j = half * (PACK // 2) + i
-                nc.scalar.activation(
-                    out=scaled[:, i, :],
-                    in_=x_sb[:, b, c, j, :],
-                    func=mybir.ActivationFunctionType.Copy,
-                    scale=diag[:, b, c, j : j + 1],
+            for c in range(PASSES):
+                scaled = keep.tile([P, PACK, SIGNAL], F32, name="scaled%d_%d" % (b, c))
+                for j in range(PACK):
+                    nc.scalar.activation(
+                        out=scaled[:, j, :],
+                        in_=x_sb[:, b, c, j, :],
+                        func=mybir.ActivationFunctionType.Copy,
+                        scale=diag[:, b, c, j : j + 1],
+                    )
+                nc.sync.dma_start(
+                    out=out[0, b].rearrange("(c p j) f t -> c p (j f t)", p=P, j=PACK)[c],
+                    in_=scaled[:].rearrange("p j s -> p (j s)"),
                 )
-            rows = out[0, b].rearrange("(c p h i) f t -> c h p (i f t)", p=P, h=2, i=PACK // 2)
-            nc.sync.dma_start(out=rows[c, half], in_=scaled[:].rearrange("p i s -> p (i s)"))
 
         def multiply(c, b, k, u):
             cols = slice(u * UNIT, (u + 1) * UNIT)
@@ -150,72 +140,63 @@ def tile_napl_conv_withsat_pb_kernel(tc, supports, cheb_2, spatial_attention, x,
             regroup(nc.scalar.copy, grouped[:, split:, :], product[:, :, split:])
             return grouped
 
-        def quantise(c, b, k, u, grouped):
-            cols = slice(u * UNIT, (u + 1) * UNIT)
+        def quantise(c, b, k, first, grouped):
+            cols = slice(first, first + grouped.shape[1])
             nc.vector.quantize_mx(
                 out=codes[b, k][:, c, cols].bitcast(FP8X4),
                 scales=scales[b, k][:, c, cols],
-                in_=grouped[:].rearrange("p w j -> p (w j)"),
+                in_=grouped.rearrange("p w j -> p (w j)"),
             )
 
-        def contract(b, k, u):
-            banks = []
-            for bank in range(UNIT // (BANK_TILES * M_TILE)):
-                acc = psum.tile([P, BANK_TILES, SIGNAL], F32)
-                for i in range(BANK_TILES):
-                    first = u * UNIT + (bank * BANK_TILES + i) * M_TILE
-                    m_cols = slice(first, first + M_TILE)
-                    for c in range(PASSES):
-                        nc.tensor.matmul_mx(
-                            out=acc[:, i, :],
-                            lhsT=codes[b, k][:, c, m_cols].bitcast(FP8X4),
-                            lhsT_scale=scales[b, k][:, c, m_cols],
-                            rhs=x_codes[:, b, c, :].bitcast(FP8X4),
-                            rhs_scale=x_scales[:, b, c, :],
-                            start=(c == 0),
-                            stop=(c == PASSES - 1),
-                        )
-                banks.append(acc)
-            return banks
+        def contract(b, k, first):
+            acc = psum.tile([P, BANK_TILES, SIGNAL], F32)
+            for i in range(BANK_TILES):
+                m_cols = slice(first + i * M_TILE, first + (i + 1) * M_TILE)
+                for c in range(PASSES):
+                    nc.tensor.matmul_mx(
+                        out=acc[:, i, :],
+                        lhsT=codes[b, k][:, c, m_cols].bitcast(FP8X4),
+                        lhsT_scale=scales[b, k][:, c, m_cols],
+                        rhs=x_codes[:, b, c, :].bitcast(FP8X4),
+                        rhs_scale=x_scales[:, b, c, :],
+                        start=(c == 0),
+                        stop=(c == LAST),
+                    )
+            return acc
 
-        def empty_and_store(b, k, u, banks):
-            result = keep.tile(
-                [P, UNIT // M_TILE, SIGNAL], F32, name="result%d_%d_%d" % (b, k, u)
-            )
-            for bank, acc in enumerate(banks):
-                nc.scalar.copy(
-                    out=result[:, bank * BANK_TILES : (bank + 1) * BANK_TILES, :], in_=acc[:]
-                )
-            rows = out[1 + k, b].rearrange("(u t p) f s -> u p t (f s)", t=UNIT // M_TILE, p=P)
-            nc.sync.dma_start(out=rows[u], in_=result[:])
+        def empty_and_store(b, k, first, acc):
+            result = keep.tile([P, BANK_TILES, SIGNAL], F32, name="result%d_%d_%d" % (b, k, first))
+            nc.scalar.copy(out=result[:], in_=acc[:])
+            rows = out[1 + k, b, first : first + BANK_COLS]
+            nc.sync.dma_start(out=rows.rearrange("(t p) f s -> p t (f s)", p=P), in_=result[:])
 
         rounds = []
         for c in range(PASSES):
-            for b in range(SAMPLES):
-                for u in range(UNITS):
+            for u in range(UNITS):
+                for b in range(SAMPLES):
                     for k in range(TERMS):
                         rounds.append((c, b, k, u))
 
-        products = {}
+        products = {0: multiply(*rounds[0])}
         groupeds = {}
         sums = {}
-        for s in range(-1, len(rounds) + 2):
-            if 0 <= s < len(rounds):
-                c, b, k, u = rounds[s]
-                if c == 0:
-                    scale_rows(b, k, u)
-                groupeds[s] = regroup_product(c, products[s])
+        for s in range(len(rounds) + 2):
+            if s < len(rounds):
+                groupeds[s] = regroup_product(rounds[s][0], products[s])
             if s + 1 < len(rounds):
-                c, b, k, u = rounds[s + 1]
-                if (c, k, u) == (0, 0, 0):
-                    quantise_signal(b)
-                    widen_diagonal(b)
-                products[s + 1] = multiply(c, b, k, u)
+                products[s + 1] = multiply(*rounds[s + 1])
             if 0 <= s - 1 < len(rounds):
                 c, b, k, u = rounds[s - 1]
-                quantise(c, b, k, u, groupeds[s - 1])
-                if c == PASSES - 1:
-                    sums[s - 1] = contract(b, k, u)
+                if c < LAST:
+                    quantise(c, b, k, u * UNIT, groupeds[s - 1][:])
+                else:
+                    sums[s - 1] = []
+                    for i in range(BANKS):
+                        first = u * UNIT + i * BANK_COLS
+                        part = groupeds[s - 1][:, i * BANK_COLS : (i + 1) * BANK_COLS, :]
+                        quantise(c, b, k, first, part)
+                        sums[s - 1].append(contract(b, k, first))
             if s - 2 in sums:
                 c, b, k, u = rounds[s - 2]
-                empty_and_store(b, k, u, sums[s - 2])
+                for i in range(BANKS):
+                    empty_and_store(b, k, u * UNIT + i * BANK_COLS, sums[s - 2][i])

@@ -1,5 +1,6 @@
 from contextlib import ExitStack
 
+import concourse.masks as masks
 import concourse.mybir as mybir
 
 BF16 = mybir.dt.bfloat16
@@ -24,7 +25,7 @@ BANK_COLS = BANK_TILES * M_TILE
 BANKS = UNIT // BANK_COLS
 RUN = 4
 BLOCK = 16
-VECTOR_COLS = (96, 256)
+VECTOR_COLS = (96, 256, 0, 256)
 
 FLOPS = 2 * TERMS * SAMPLES * NODES * NODES * SIGNAL
 
@@ -68,6 +69,11 @@ def tile_napl_conv_withsat_pb_kernel(tc, supports, cheb_2, spatial_attention, x,
         x_scales = keep.tile([P, SAMPLES, PASSES, SIGNAL], U8, align_bytes=64)
         diag_bf = keep.tile([P, SAMPLES, PASSES, BLOCK], BF16)
         diag = keep.tile([P, SAMPLES, PASSES, PACK], F32)
+        identity = keep.tile([P, P], BF16)
+        masks.make_identity(nc, identity[:])
+        att_grouped = {}
+        for b in range(SAMPLES):
+            att_grouped[b] = keep.tile([P, UNIT, PACK], BF16, name="att_grouped%d" % b)
 
         def load_columns(slab, matrix, c, cols):
             rows = matrix[c * P * PACK : (c + 1) * P * PACK, :]
@@ -96,7 +102,10 @@ def tile_napl_conv_withsat_pb_kernel(tc, supports, cheb_2, spatial_attention, x,
                     )
         for u in range(UNITS):
             load_matrices(0, slice(u * UNIT, (u + 1) * UNIT))
-        load_matrices(LAST, slice(0, NODES))
+        for b in range(SAMPLES):
+            load_columns(att_sb[b, LAST], spatial_attention[b], LAST, slice(0, NODES))
+        for k in range(TERMS):
+            load_columns(term_sb[k, LAST], terms[k], LAST, slice(0, NODES))
 
         for b in range(SAMPLES):
             for c in range(PASSES):
@@ -133,10 +142,37 @@ def tile_napl_conv_withsat_pb_kernel(tc, supports, cheb_2, spatial_attention, x,
             )
             return product
 
-        def regroup_product(c, product):
-            split = VECTOR_COLS[c]
-            grouped = stage.tile([P, UNIT, PACK], BF16, align_bytes=64)
-            regroup(nc.vector.tensor_copy, grouped[:, :split, :], product[:, :, :split])
+        def interleave_on_tensor(k, c, first):
+            bank = psum.tile([P, BANK_COLS, PACK], BF16, name="acc")
+            for i in range(BANK_TILES):
+                nc.tensor.matmul(
+                    out=bank[:, i * M_TILE : (i + 1) * M_TILE, :],
+                    lhsT=identity[:],
+                    rhs=term_sb[k, c][
+                        :, :, first + i * M_TILE : first + (i + 1) * M_TILE
+                    ].rearrange("p j w -> p w j"),
+                    start=True,
+                    stop=True,
+                )
+            return bank
+
+        def multiply_grouped(b, banks):
+            grouped = stage.tile([P, UNIT, PACK], BF16, align_bytes=64, name="grouped")
+            for i in range(BANKS):
+                cols = slice(i * BANK_COLS, (i + 1) * BANK_COLS)
+                nc.vector.tensor_tensor(
+                    out=grouped[:, cols, :],
+                    in0=banks[i][:],
+                    in1=att_grouped[b][:, cols, :],
+                    op=mybir.AluOpType.mult,
+                )
+            return grouped
+
+        def regroup_product(phase, product):
+            split = VECTOR_COLS[phase]
+            grouped = stage.tile([P, UNIT, PACK], BF16, align_bytes=64, name="grouped")
+            if split:
+                regroup(nc.vector.tensor_copy, grouped[:, :split, :], product[:, :, :split])
             regroup(nc.scalar.copy, grouped[:, split:, :], product[:, :, split:])
             return grouped
 
@@ -149,7 +185,7 @@ def tile_napl_conv_withsat_pb_kernel(tc, supports, cheb_2, spatial_attention, x,
             )
 
         def contract(b, k, first):
-            acc = psum.tile([P, BANK_TILES, SIGNAL], F32)
+            acc = psum.tile([P, BANK_TILES, SIGNAL], F32, name="acc")
             for i in range(BANK_TILES):
                 m_cols = slice(first + i * M_TILE, first + (i + 1) * M_TILE)
                 for c in range(PASSES):
@@ -177,13 +213,28 @@ def tile_napl_conv_withsat_pb_kernel(tc, supports, cheb_2, spatial_attention, x,
                     for k in range(TERMS):
                         rounds.append((c, b, k, u))
 
+        def on_tensor(s):
+            return 8 <= s < 12
+
+        term_grouped = {}
         products = {0: multiply(*rounds[0])}
         groupeds = {}
         sums = {}
         for s in range(len(rounds) + 2):
             if s < len(rounds):
-                groupeds[s] = regroup_product(rounds[s][0], products[s])
-            if s + 1 < len(rounds):
+                if on_tensor(s):
+                    groupeds[s] = multiply_grouped(rounds[s][1], term_grouped[rounds[s][2]])
+                else:
+                    groupeds[s] = regroup_product(s // 4, products[s])
+            if 4 <= s < 8:
+                b, half = divmod(s - 4, 2)
+                cols = slice(half * BANK_COLS, (half + 1) * BANK_COLS)
+                regroup(nc.scalar.copy, att_grouped[b][:, cols, :], att_sb[b, LAST][:, :, cols])
+            if 6 <= s < 8:
+                term_grouped[s - 6] = [
+                    interleave_on_tensor(s - 6, LAST, i * BANK_COLS) for i in range(BANKS)
+                ]
+            if s + 1 < len(rounds) and not on_tensor(s + 1):
                 products[s + 1] = multiply(*rounds[s + 1])
             if 0 <= s - 1 < len(rounds):
                 c, b, k, u = rounds[s - 1]

@@ -25,7 +25,9 @@ BANK_COLS = BANK_TILES * M_TILE
 BANKS = UNIT // BANK_COLS
 RUN = 4
 BLOCK = 16
-VECTOR_COLS = (96, 256, 0, 256)
+TENSOR_UNIT = 1
+VECTOR_COLS = (96, 96, 416, 0)
+QUARTER = SAMPLES * TERMS
 
 FLOPS = 2 * TERMS * SAMPLES * NODES * NODES * SIGNAL
 
@@ -43,13 +45,15 @@ def tile_napl_conv_withsat_pb_kernel(tc, supports, cheb_2, spatial_attention, x,
     with ExitStack() as ctx:
         keep = ctx.enter_context(tc.tile_pool(name="keep", bufs=1))
         stage = ctx.enter_context(tc.tile_pool(name="stage", bufs=3))
-        psum = ctx.enter_context(tc.psum_pool(name="psum", bufs=8))
+        psum = ctx.enter_context(tc.psum_pool(name="psum", bufs=4))
+        psum_terms = ctx.enter_context(tc.psum_pool(name="psum_terms", bufs=4))
         ctx.enter_context(tc.manual_schedule())
 
         term_sb = {}
         att_sb = {}
         codes = {}
         scales = {}
+        att_grouped = {}
         for c in range(PASSES):
             for k in range(TERMS):
                 term_sb[k, c] = keep.tile([P, PACK, NODES], BF16, name="term%d_%d" % (k, c))
@@ -63,6 +67,7 @@ def tile_napl_conv_withsat_pb_kernel(tc, supports, cheb_2, spatial_attention, x,
                 scales[b, k] = keep.tile(
                     [P, PASSES, NODES], U8, name="scales%d_%d" % (b, k), align_bytes=64
                 )
+            att_grouped[b] = keep.tile([P, UNIT, PACK], BF16, name="att_grouped%d" % b)
         x_sb = keep.tile([P, SAMPLES, PASSES, PACK, SIGNAL], BF16)
         x_grouped = keep.tile([P, SAMPLES, PASSES, SIGNAL, PACK], BF16, align_bytes=64)
         x_codes = keep.tile([P, SAMPLES, PASSES, SIGNAL], U32, align_bytes=64)
@@ -71,21 +76,12 @@ def tile_napl_conv_withsat_pb_kernel(tc, supports, cheb_2, spatial_attention, x,
         diag = keep.tile([P, SAMPLES, PASSES, PACK], F32)
         identity = keep.tile([P, P], BF16)
         masks.make_identity(nc, identity[:])
-        att_grouped = {}
-        for b in range(SAMPLES):
-            att_grouped[b] = keep.tile([P, UNIT, PACK], BF16, name="att_grouped%d" % b)
 
         def load_columns(slab, matrix, c, cols):
             rows = matrix[c * P * PACK : (c + 1) * P * PACK, :]
             nc.sync.dma_start(
                 out=slab[:, :, cols], in_=rows.rearrange("(p j) m -> p j m", j=PACK)[:, :, cols]
             )
-
-        def load_matrices(c, cols):
-            load_columns(term_sb[0, c], terms[0], c, cols)
-            load_columns(att_sb[0, c], spatial_attention[0], c, cols)
-            load_columns(term_sb[1, c], terms[1], c, cols)
-            load_columns(att_sb[1, c], spatial_attention[1], c, cols)
 
         for b in range(SAMPLES):
             nc.sync.dma_start(
@@ -101,11 +97,14 @@ def tile_napl_conv_withsat_pb_kernel(tc, supports, cheb_2, spatial_attention, x,
                         in_=on_diagonal.rearrange("(c p j) -> c p j", p=P, j=PACK)[c],
                     )
         for u in range(UNITS):
-            load_matrices(0, slice(u * UNIT, (u + 1) * UNIT))
-        for b in range(SAMPLES):
-            load_columns(att_sb[b, LAST], spatial_attention[b], LAST, slice(0, NODES))
-        for k in range(TERMS):
-            load_columns(term_sb[k, LAST], terms[k], LAST, slice(0, NODES))
+            cols = slice(u * UNIT, (u + 1) * UNIT)
+            load_columns(term_sb[0, 0], terms[0], 0, cols)
+            load_columns(att_sb[0, 0], spatial_attention[0], 0, cols)
+            load_columns(term_sb[1, 0], terms[1], 0, cols)
+            load_columns(att_sb[1, 0], spatial_attention[1], 0, cols)
+        for i in range(SAMPLES):
+            load_columns(term_sb[i, LAST], terms[i], LAST, slice(0, NODES))
+            load_columns(att_sb[i, LAST], spatial_attention[i], LAST, slice(0, NODES))
 
         for b in range(SAMPLES):
             for c in range(PASSES):
@@ -131,49 +130,71 @@ def tile_napl_conv_withsat_pb_kernel(tc, supports, cheb_2, spatial_attention, x,
                     in_=scaled[:].rearrange("p j s -> p (j s)"),
                 )
 
-        def multiply(c, b, k, u):
-            cols = slice(u * UNIT, (u + 1) * UNIT)
-            product = stage.tile([P, PACK, UNIT], BF16)
+        rounds = []
+        for c in range(PASSES):
+            for u in range(UNITS):
+                for b in range(SAMPLES):
+                    for k in range(TERMS):
+                        rounds.append((c, b, k, u))
+
+        def tensor_cols(s):
+            c, b, k, u = rounds[s]
+            return UNIT if c == LAST and u == TENSOR_UNIT else 0
+
+        term_grouped = {}
+
+        def interleave_term(k, first):
+            bank = psum_terms.tile([P, BANK_COLS, PACK], BF16, name="bank")
+            for i in range(BANK_TILES):
+                start = TENSOR_UNIT * UNIT + first + i * M_TILE
+                cols = slice(start, start + M_TILE)
+                nc.tensor.matmul(
+                    out=bank[:, i * M_TILE : (i + 1) * M_TILE, :],
+                    lhsT=identity[:],
+                    rhs=term_sb[k, LAST][:, :, cols].rearrange("p j w -> p w j"),
+                    start=True,
+                    stop=True,
+                )
+            term_grouped[k, first] = bank
+
+        def regroup_attention(b, first, width):
+            start = TENSOR_UNIT * UNIT + first
+            regroup(
+                nc.scalar.copy,
+                att_grouped[b][:, first : first + width, :],
+                att_sb[b, LAST][:, :, start : start + width],
+            )
+
+        def multiply(s):
+            c, b, k, u = rounds[s]
+            cols = slice(u * UNIT + tensor_cols(s), (u + 1) * UNIT)
+            product = stage.tile([P, PACK, UNIT], BF16, name="product")
             nc.vector.tensor_tensor(
-                out=product[:],
+                out=product[:, :, tensor_cols(s) :],
                 in0=term_sb[k, c][:, :, cols],
                 in1=att_sb[b, c][:, :, cols],
                 op=mybir.AluOpType.mult,
             )
             return product
 
-        def interleave_on_tensor(k, c, first):
-            bank = psum.tile([P, BANK_COLS, PACK], BF16, name="acc")
-            for i in range(BANK_TILES):
-                nc.tensor.matmul(
-                    out=bank[:, i * M_TILE : (i + 1) * M_TILE, :],
-                    lhsT=identity[:],
-                    rhs=term_sb[k, c][
-                        :, :, first + i * M_TILE : first + (i + 1) * M_TILE
-                    ].rearrange("p j w -> p w j"),
-                    start=True,
-                    stop=True,
-                )
-            return bank
-
-        def multiply_grouped(b, banks):
+        def group(s, product):
+            c, b, k, u = rounds[s]
             grouped = stage.tile([P, UNIT, PACK], BF16, align_bytes=64, name="grouped")
-            for i in range(BANKS):
-                cols = slice(i * BANK_COLS, (i + 1) * BANK_COLS)
+            for first in range(0, tensor_cols(s), BANK_COLS):
                 nc.vector.tensor_tensor(
-                    out=grouped[:, cols, :],
-                    in0=banks[i][:],
-                    in1=att_grouped[b][:, cols, :],
+                    out=grouped[:, first : first + BANK_COLS, :],
+                    in0=term_grouped[k, first][:],
+                    in1=att_grouped[b][:, first : first + BANK_COLS, :],
                     op=mybir.AluOpType.mult,
                 )
-            return grouped
-
-        def regroup_product(phase, product):
-            split = VECTOR_COLS[phase]
-            grouped = stage.tile([P, UNIT, PACK], BF16, align_bytes=64, name="grouped")
-            if split:
-                regroup(nc.vector.tensor_copy, grouped[:, :split, :], product[:, :, :split])
-            regroup(nc.scalar.copy, grouped[:, split:, :], product[:, :, split:])
+            if tensor_cols(s) < UNIT:
+                split = tensor_cols(s) + VECTOR_COLS[s // QUARTER]
+                regroup(
+                    nc.vector.tensor_copy,
+                    grouped[:, tensor_cols(s) : split, :],
+                    product[:, :, tensor_cols(s) : split],
+                )
+                regroup(nc.scalar.copy, grouped[:, split:, :], product[:, :, split:])
             return grouped
 
         def quantise(c, b, k, first, grouped):
@@ -185,7 +206,7 @@ def tile_napl_conv_withsat_pb_kernel(tc, supports, cheb_2, spatial_attention, x,
             )
 
         def contract(b, k, first):
-            acc = psum.tile([P, BANK_TILES, SIGNAL], F32, name="acc")
+            acc = psum.tile([P, BANK_TILES, SIGNAL], F32, name="bank")
             for i in range(BANK_TILES):
                 m_cols = slice(first + i * M_TILE, first + (i + 1) * M_TILE)
                 for c in range(PASSES):
@@ -206,36 +227,25 @@ def tile_napl_conv_withsat_pb_kernel(tc, supports, cheb_2, spatial_attention, x,
             rows = out[1 + k, b, first : first + BANK_COLS]
             nc.sync.dma_start(out=rows.rearrange("(t p) f s -> p t (f s)", p=P), in_=result[:])
 
-        rounds = []
-        for c in range(PASSES):
-            for u in range(UNITS):
-                for b in range(SAMPLES):
-                    for k in range(TERMS):
-                        rounds.append((c, b, k, u))
+        attention_jobs = {}
+        for b in range(SAMPLES):
+            for i in range(BANKS):
+                attention_jobs[2 * QUARTER + BANKS * b + i] = (b, i * BANK_COLS, BANK_COLS)
+        term_jobs = {
+            2 * QUARTER - 2: [(0, 0), (0, BANK_COLS)],
+            2 * QUARTER - 1: [(1, 0), (1, BANK_COLS)],
+        }
 
-        def on_tensor(s):
-            return 8 <= s < 12
-
-        term_grouped = {}
-        products = {0: multiply(*rounds[0])}
+        products = {0: multiply(0)}
         groupeds = {}
         sums = {}
         for s in range(len(rounds) + 2):
             if s < len(rounds):
-                if on_tensor(s):
-                    groupeds[s] = multiply_grouped(rounds[s][1], term_grouped[rounds[s][2]])
-                else:
-                    groupeds[s] = regroup_product(s // 4, products[s])
-            if 4 <= s < 8:
-                b, half = divmod(s - 4, 2)
-                cols = slice(half * BANK_COLS, (half + 1) * BANK_COLS)
-                regroup(nc.scalar.copy, att_grouped[b][:, cols, :], att_sb[b, LAST][:, :, cols])
-            if 6 <= s < 8:
-                term_grouped[s - 6] = [
-                    interleave_on_tensor(s - 6, LAST, i * BANK_COLS) for i in range(BANKS)
-                ]
-            if s + 1 < len(rounds) and not on_tensor(s + 1):
-                products[s + 1] = multiply(*rounds[s + 1])
+                groupeds[s] = group(s, products.get(s))
+            if s in attention_jobs:
+                regroup_attention(*attention_jobs[s])
+            if s + 1 < len(rounds) and tensor_cols(s + 1) < UNIT:
+                products[s + 1] = multiply(s + 1)
             if 0 <= s - 1 < len(rounds):
                 c, b, k, u = rounds[s - 1]
                 if c < LAST:
@@ -247,6 +257,8 @@ def tile_napl_conv_withsat_pb_kernel(tc, supports, cheb_2, spatial_attention, x,
                         part = groupeds[s - 1][:, i * BANK_COLS : (i + 1) * BANK_COLS, :]
                         quantise(c, b, k, first, part)
                         sums[s - 1].append(contract(b, k, first))
+            for k, first in term_jobs.get(s, []):
+                interleave_term(k, first)
             if s - 2 in sums:
                 c, b, k, u = rounds[s - 2]
                 for i in range(BANKS):

@@ -25,8 +25,8 @@ BANK_COLS = BANK_TILES * M_TILE
 BANKS = UNIT // BANK_COLS
 RUN = 4
 BLOCK = 16
-TENSOR_UNIT = 1
-VECTOR_COLS = (96, 96, 416, 0)
+TENSOR_COLS = (0, 256, 256, 256)
+VECTOR_COLS = (112, 0, 160, 128)
 QUARTER = SAMPLES * TERMS
 
 FLOPS = 2 * TERMS * SAMPLES * NODES * NODES * SIGNAL
@@ -67,7 +67,10 @@ def tile_napl_conv_withsat_pb_kernel(tc, supports, cheb_2, spatial_attention, x,
                 scales[b, k] = keep.tile(
                     [P, PASSES, NODES], U8, name="scales%d_%d" % (b, k), align_bytes=64
                 )
-            att_grouped[b] = keep.tile([P, UNIT, PACK], BF16, name="att_grouped%d" % b)
+            for q in range(1, PASSES * UNITS):
+                att_grouped[b, q] = keep.tile(
+                    [P, BANK_COLS, PACK], BF16, name="att_grouped%d_%d" % (b, q)
+                )
         x_sb = keep.tile([P, SAMPLES, PASSES, PACK, SIGNAL], BF16)
         x_grouped = keep.tile([P, SAMPLES, PASSES, SIGNAL, PACK], BF16, align_bytes=64)
         x_codes = keep.tile([P, SAMPLES, PASSES, SIGNAL], U32, align_bytes=64)
@@ -138,31 +141,30 @@ def tile_napl_conv_withsat_pb_kernel(tc, supports, cheb_2, spatial_attention, x,
                         rounds.append((c, b, k, u))
 
         def tensor_cols(s):
-            c, b, k, u = rounds[s]
-            return UNIT if c == LAST and u == TENSOR_UNIT else 0
+            return TENSOR_COLS[s // QUARTER]
 
         term_grouped = {}
 
-        def interleave_term(k, first):
-            bank = psum_terms.tile([P, BANK_COLS, PACK], BF16, name="bank")
+        def interleave_term(pool, k, q):
+            c, u = divmod(q, UNITS)
+            bank = pool.tile([P, BANK_COLS, PACK], BF16, name="bank")
             for i in range(BANK_TILES):
-                start = TENSOR_UNIT * UNIT + first + i * M_TILE
-                cols = slice(start, start + M_TILE)
+                cols = slice(u * UNIT + i * M_TILE, u * UNIT + (i + 1) * M_TILE)
                 nc.tensor.matmul(
                     out=bank[:, i * M_TILE : (i + 1) * M_TILE, :],
                     lhsT=identity[:],
-                    rhs=term_sb[k, LAST][:, :, cols].rearrange("p j w -> p w j"),
+                    rhs=term_sb[k, c][:, :, cols].rearrange("p j w -> p w j"),
                     start=True,
                     stop=True,
                 )
-            term_grouped[k, first] = bank
+            term_grouped[k, q] = bank
 
-        def regroup_attention(b, first, width):
-            start = TENSOR_UNIT * UNIT + first
+        def regroup_attention(b, q, i):
+            c, u = divmod(q, UNITS)
             regroup(
                 nc.scalar.copy,
-                att_grouped[b][:, first : first + width, :],
-                att_sb[b, LAST][:, :, start : start + width],
+                att_grouped[b, q][:, i * M_TILE : (i + 1) * M_TILE, :],
+                att_sb[b, c][:, :, u * UNIT + i * M_TILE : u * UNIT + (i + 1) * M_TILE],
             )
 
         def multiply(s):
@@ -180,21 +182,21 @@ def tile_napl_conv_withsat_pb_kernel(tc, supports, cheb_2, spatial_attention, x,
         def group(s, product):
             c, b, k, u = rounds[s]
             grouped = stage.tile([P, UNIT, PACK], BF16, align_bytes=64, name="grouped")
-            for first in range(0, tensor_cols(s), BANK_COLS):
+            if tensor_cols(s):
                 nc.vector.tensor_tensor(
-                    out=grouped[:, first : first + BANK_COLS, :],
-                    in0=term_grouped[k, first][:],
-                    in1=att_grouped[b][:, first : first + BANK_COLS, :],
+                    out=grouped[:, : tensor_cols(s), :],
+                    in0=term_grouped[k, s // QUARTER][:],
+                    in1=att_grouped[b, s // QUARTER][:],
                     op=mybir.AluOpType.mult,
                 )
-            if tensor_cols(s) < UNIT:
-                split = tensor_cols(s) + VECTOR_COLS[s // QUARTER]
+            split = tensor_cols(s) + VECTOR_COLS[s // QUARTER]
+            if split > tensor_cols(s):
                 regroup(
                     nc.vector.tensor_copy,
                     grouped[:, tensor_cols(s) : split, :],
                     product[:, :, tensor_cols(s) : split],
                 )
-                regroup(nc.scalar.copy, grouped[:, split:, :], product[:, :, split:])
+            regroup(nc.scalar.copy, grouped[:, split:, :], product[:, :, split:])
             return grouped
 
         def quantise(c, b, k, first, grouped):
@@ -228,23 +230,24 @@ def tile_napl_conv_withsat_pb_kernel(tc, supports, cheb_2, spatial_attention, x,
             nc.sync.dma_start(out=rows.rearrange("(t p) f s -> p t (f s)", p=P), in_=result[:])
 
         attention_jobs = {}
-        for b in range(SAMPLES):
-            for i in range(BANKS):
-                attention_jobs[2 * QUARTER + BANKS * b + i] = (b, i * BANK_COLS, BANK_COLS)
+        for q in range(1, PASSES * UNITS):
+            for b in range(SAMPLES):
+                for i in range(BANK_TILES):
+                    attention_jobs[QUARTER * q + TERMS * b - BANK_TILES + i] = (b, q, i)
         term_jobs = {
-            2 * QUARTER - 2: [(0, 0), (0, BANK_COLS)],
-            2 * QUARTER - 1: [(1, 0), (1, BANK_COLS)],
+            1: [(psum, 0, 1), (psum, 1, 1)],
+            QUARTER: [(psum_terms, 0, 2), (psum_terms, 0, 3), (psum_terms, 1, 2), (psum_terms, 1, 3)],
         }
 
         products = {0: multiply(0)}
         groupeds = {}
         sums = {}
         for s in range(len(rounds) + 2):
-            if s < len(rounds):
-                groupeds[s] = group(s, products.get(s))
             if s in attention_jobs:
                 regroup_attention(*attention_jobs[s])
-            if s + 1 < len(rounds) and tensor_cols(s + 1) < UNIT:
+            if s < len(rounds):
+                groupeds[s] = group(s, products[s])
+            if s + 1 < len(rounds):
                 products[s + 1] = multiply(s + 1)
             if 0 <= s - 1 < len(rounds):
                 c, b, k, u = rounds[s - 1]
@@ -257,8 +260,8 @@ def tile_napl_conv_withsat_pb_kernel(tc, supports, cheb_2, spatial_attention, x,
                         part = groupeds[s - 1][:, i * BANK_COLS : (i + 1) * BANK_COLS, :]
                         quantise(c, b, k, first, part)
                         sums[s - 1].append(contract(b, k, first))
-            for k, first in term_jobs.get(s, []):
-                interleave_term(k, first)
+            for pool, k, q in term_jobs.get(s, []):
+                interleave_term(pool, k, q)
             if s - 2 in sums:
                 c, b, k, u = rounds[s - 2]
                 for i in range(BANKS):

@@ -207,26 +207,30 @@ def tile_napl_conv_withsat_pb_kernel(tc, supports, cheb_2, spatial_attention, x,
                 in_=grouped.rearrange("p w j -> p (w j)"),
             )
 
+        def add_pass(sums_of_tile, b, k, c, first):
+            m_cols = slice(first, first + M_TILE)
+            nc.tensor.matmul_mx(
+                out=sums_of_tile,
+                lhsT=codes[b, k][:, c, m_cols].bitcast(FP8X4),
+                lhsT_scale=scales[b, k][:, c, m_cols],
+                rhs=x_codes[:, b, c, :].bitcast(FP8X4),
+                rhs_scale=x_scales[:, b, c, :],
+                start=(c == 0),
+                stop=(c == LAST),
+            )
+
         def contract(b, k, first):
             acc = psum.tile([P, BANK_TILES, SIGNAL], F32, name="bank")
             for i in range(BANK_TILES):
-                m_cols = slice(first + i * M_TILE, first + (i + 1) * M_TILE)
                 for c in range(PASSES):
-                    nc.tensor.matmul_mx(
-                        out=acc[:, i, :],
-                        lhsT=codes[b, k][:, c, m_cols].bitcast(FP8X4),
-                        lhsT_scale=scales[b, k][:, c, m_cols],
-                        rhs=x_codes[:, b, c, :].bitcast(FP8X4),
-                        rhs_scale=x_scales[:, b, c, :],
-                        start=(c == 0),
-                        stop=(c == LAST),
-                    )
+                    add_pass(acc[:, i, :], b, k, c, first + i * M_TILE)
             return acc
 
-        def empty_and_store(b, k, first, acc):
-            result = keep.tile([P, BANK_TILES, SIGNAL], F32, name="result%d_%d_%d" % (b, k, first))
-            nc.scalar.copy(out=result[:], in_=acc[:])
-            rows = out[1 + k, b, first : first + BANK_COLS]
+        def empty_and_store(engine_copy, b, k, first, acc):
+            tiles = acc.shape[1]
+            result = keep.tile([P, tiles, SIGNAL], F32, name="result%d_%d_%d" % (b, k, first))
+            engine_copy(out=result[:], in_=acc)
+            rows = out[1 + k, b, first : first + tiles * M_TILE]
             nc.sync.dma_start(out=rows.rearrange("(t p) f s -> p t (f s)", p=P), in_=result[:])
 
         attention_jobs = {}
@@ -239,30 +243,69 @@ def tile_napl_conv_withsat_pb_kernel(tc, supports, cheb_2, spatial_attention, x,
             QUARTER: [(psum_terms, 0, 2), (psum_terms, 0, 3), (psum_terms, 1, 2), (psum_terms, 1, 3)],
         }
 
+        def quantise_and_contract(s):
+            c, b, k, u = rounds[s]
+            if c < LAST:
+                quantise(c, b, k, u * UNIT, groupeds[s][:])
+                return []
+            banks = []
+            for i in range(BANKS):
+                first = u * UNIT + i * BANK_COLS
+                quantise(c, b, k, first, groupeds[s][:, i * BANK_COLS : (i + 1) * BANK_COLS, :])
+                banks.append(contract(b, k, first))
+            return banks
+
+        def empty_round(s, engine_copies):
+            c, b, k, u = rounds[s]
+            for i in range(len(sums[s])):
+                empty_and_store(engine_copies[i], b, k, u * UNIT + i * BANK_COLS, sums[s][i][:])
+
+        final = len(rounds) - 1
         products = {0: multiply(0)}
         groupeds = {}
         sums = {}
-        for s in range(len(rounds) + 2):
+        for s in range(final - 1):
             if s in attention_jobs:
                 regroup_attention(*attention_jobs[s])
-            if s < len(rounds):
-                groupeds[s] = group(s, products[s])
-            if s + 1 < len(rounds):
-                products[s + 1] = multiply(s + 1)
-            if 0 <= s - 1 < len(rounds):
-                c, b, k, u = rounds[s - 1]
-                if c < LAST:
-                    quantise(c, b, k, u * UNIT, groupeds[s - 1][:])
-                else:
-                    sums[s - 1] = []
-                    for i in range(BANKS):
-                        first = u * UNIT + i * BANK_COLS
-                        part = groupeds[s - 1][:, i * BANK_COLS : (i + 1) * BANK_COLS, :]
-                        quantise(c, b, k, first, part)
-                        sums[s - 1].append(contract(b, k, first))
+            groupeds[s] = group(s, products[s])
+            products[s + 1] = multiply(s + 1)
+            if s >= 1:
+                sums[s - 1] = quantise_and_contract(s - 1)
             for pool, k, q in term_jobs.get(s, []):
                 interleave_term(pool, k, q)
-            if s - 2 in sums:
-                c, b, k, u = rounds[s - 2]
-                for i in range(BANKS):
-                    empty_and_store(b, k, u * UNIT + i * BANK_COLS, sums[s - 2][i])
+            if s >= 2:
+                empty_round(s - 2, (nc.scalar.copy, nc.scalar.copy))
+
+        groupeds[final - 1] = group(final - 1, products[final - 1])
+        sums[final - 2] = quantise_and_contract(final - 2)
+        products[final] = multiply(final)
+        empty_round(final - 3, (nc.scalar.copy, nc.scalar.copy))
+        c, b, k, u = rounds[final]
+        tiles = UNIT // M_TILE
+        final_sums = []
+
+        def open_final_sum():
+            i = len(final_sums)
+            final_sums.append(psum_terms.tile([P, BANK_TILES, SIGNAL], F32, name="bank"))
+            add_pass(final_sums[i][:, 0, :], b, k, 0, u * UNIT + i * M_TILE)
+
+        for i in range(tiles - 1):
+            open_final_sum()
+        sums[final - 1] = quantise_and_contract(final - 1)
+        groupeds[final] = group(final, products[final])
+        open_final_sum()
+        empty_round(final - 2, (nc.scalar.copy, nc.scalar.copy))
+        for i in range(BANKS):
+            first = u * UNIT + i * BANK_COLS
+            quantise(c, b, k, first, groupeds[final][:, i * BANK_COLS : (i + 1) * BANK_COLS, :])
+            for t in range(i * BANK_TILES, (i + 1) * BANK_TILES):
+                add_pass(final_sums[t][:, 0, :], b, k, LAST, u * UNIT + t * M_TILE)
+        empty_round(final - 1, (nc.scalar.copy, nc.vector.tensor_copy))
+        for i in range(tiles):
+            empty_and_store(
+                (nc.scalar.copy, nc.vector.tensor_copy)[i % 2],
+                b,
+                k,
+                u * UNIT + i * M_TILE,
+                final_sums[i][:, :1, :],
+            )

@@ -87,10 +87,6 @@ def tile_napl_conv_withsat_pb_kernel(tc, supports, cheb_2, spatial_attention, x,
             )
 
         for b in range(SAMPLES):
-            nc.sync.dma_start(
-                out=x_sb[:, b].rearrange("p c j s -> p c (j s)"),
-                in_=x[b].rearrange("(c p j) f t -> p c (j f t)", p=P, j=PACK),
-            )
             flat = spatial_attention[b].rearrange("n m -> (n m)")
             on_diagonal = flat[0 : NODES * NODES : NODES + 1]
             with nc.allow_non_contiguous_dma(reason="a diagonal has no two neighbours"):
@@ -99,6 +95,11 @@ def tile_napl_conv_withsat_pb_kernel(tc, supports, cheb_2, spatial_attention, x,
                         out=diag_bf[:, b, c, :PACK],
                         in_=on_diagonal.rearrange("(c p j) -> c p j", p=P, j=PACK)[c],
                     )
+            for c in range(PASSES):
+                nc.sync.dma_start(
+                    out=x_sb[:, b, c].rearrange("p j s -> p (j s)"),
+                    in_=x[b].rearrange("(c p j) f t -> c p (j f t)", p=P, j=PACK)[c],
+                )
         for u in range(UNITS):
             cols = slice(u * UNIT, (u + 1) * UNIT)
             load_columns(term_sb[0, 0], terms[0], 0, cols)
@@ -179,7 +180,7 @@ def tile_napl_conv_withsat_pb_kernel(tc, supports, cheb_2, spatial_attention, x,
             )
             return product
 
-        def group(s, product):
+        def group(s, product, vector_cols):
             c, b, k, u = rounds[s]
             grouped = stage.tile([P, UNIT, PACK], BF16, align_bytes=64, name="grouped")
             if tensor_cols(s):
@@ -189,14 +190,15 @@ def tile_napl_conv_withsat_pb_kernel(tc, supports, cheb_2, spatial_attention, x,
                     in1=att_grouped[b, s // QUARTER][:],
                     op=mybir.AluOpType.mult,
                 )
-            split = tensor_cols(s) + VECTOR_COLS[s // QUARTER]
+            split = tensor_cols(s) + vector_cols
             if split > tensor_cols(s):
                 regroup(
                     nc.vector.tensor_copy,
                     grouped[:, tensor_cols(s) : split, :],
                     product[:, :, tensor_cols(s) : split],
                 )
-            regroup(nc.scalar.copy, grouped[:, split:, :], product[:, :, split:])
+            if split < UNIT:
+                regroup(nc.scalar.copy, grouped[:, split:, :], product[:, :, split:])
             return grouped
 
         def quantise(c, b, k, first, grouped):
@@ -267,7 +269,7 @@ def tile_napl_conv_withsat_pb_kernel(tc, supports, cheb_2, spatial_attention, x,
         for s in range(final - 1):
             if s in attention_jobs:
                 regroup_attention(*attention_jobs[s])
-            groupeds[s] = group(s, products[s])
+            groupeds[s] = group(s, products[s], VECTOR_COLS[s // QUARTER])
             products[s + 1] = multiply(s + 1)
             if s >= 1:
                 sums[s - 1] = quantise_and_contract(s - 1)
@@ -276,7 +278,7 @@ def tile_napl_conv_withsat_pb_kernel(tc, supports, cheb_2, spatial_attention, x,
             if s >= 2:
                 empty_round(s - 2, (nc.scalar.copy, nc.scalar.copy))
 
-        groupeds[final - 1] = group(final - 1, products[final - 1])
+        groupeds[final - 1] = group(final - 1, products[final - 1], VECTOR_COLS[-1])
         sums[final - 2] = quantise_and_contract(final - 2)
         products[final] = multiply(final)
         empty_round(final - 3, (nc.scalar.copy, nc.scalar.copy))
@@ -292,7 +294,7 @@ def tile_napl_conv_withsat_pb_kernel(tc, supports, cheb_2, spatial_attention, x,
         for i in range(tiles - 1):
             open_final_sum()
         sums[final - 1] = quantise_and_contract(final - 1)
-        groupeds[final] = group(final, products[final])
+        groupeds[final] = group(final, products[final], UNIT - tensor_cols(final))
         open_final_sum()
         empty_round(final - 2, (nc.scalar.copy, nc.scalar.copy))
         for i in range(BANKS):

@@ -75,7 +75,7 @@ def tile_napl_conv_withsat_pb_kernel(tc, supports, cheb_2, spatial_attention, x,
         x_grouped = keep.tile([P, SAMPLES, PASSES, SIGNAL, PACK], BF16, align_bytes=64)
         x_codes = keep.tile([P, SAMPLES, PASSES, SIGNAL], U32, align_bytes=64)
         x_scales = keep.tile([P, SAMPLES, PASSES, SIGNAL], U8, align_bytes=64)
-        diag_bf = keep.tile([P, SAMPLES, PASSES, BLOCK], BF16)
+        diag_bf = keep.tile([P, SAMPLES, PASSES, PACK, BLOCK], BF16)
         diag = keep.tile([P, SAMPLES, PASSES, PACK], F32)
         identity = keep.tile([P, P], BF16)
         masks.make_identity(nc, identity[:])
@@ -92,7 +92,7 @@ def tile_napl_conv_withsat_pb_kernel(tc, supports, cheb_2, spatial_attention, x,
             with nc.allow_non_contiguous_dma(reason="a diagonal has no two neighbours"):
                 for c in range(PASSES):
                     nc.sync.dma_start(
-                        out=diag_bf[:, b, c, :PACK],
+                        out=diag_bf[:, b, c, :, 0],
                         in_=on_diagonal.rearrange("(c p j) -> c p j", p=P, j=PACK)[c],
                     )
             for c in range(PASSES):
@@ -119,7 +119,7 @@ def tile_napl_conv_withsat_pb_kernel(tc, supports, cheb_2, spatial_attention, x,
                 in_=x_grouped[:, b].rearrange("p c s j -> p (c s j)"),
             )
 
-            nc.scalar.copy(out=diag[:, b], in_=diag_bf[:, b, :, :PACK])
+            nc.scalar.copy(out=diag[:, b], in_=diag_bf[:, b, :, :, 0])
             for c in range(PASSES):
                 scaled = keep.tile([P, PACK, SIGNAL], F32, name="scaled%d_%d" % (b, c))
                 for j in range(PACK):

@@ -26,7 +26,7 @@ BANKS = UNIT // BANK_COLS
 RUN = 4
 BLOCK = 16
 TENSOR_COLS = (0, 256, 256, 256)
-VECTOR_COLS = (112, 0, 160, 128)
+VECTOR_COLS = (144, 32, 192, 160)
 QUARTER = SAMPLES * TERMS
 
 FLOPS = 2 * TERMS * SAMPLES * NODES * NODES * SIGNAL

@@ -23,7 +23,7 @@ M_TILE = 128
 BANK_TILES = 2
 BANK_COLS = BANK_TILES * M_TILE
 BANKS = UNIT // BANK_COLS
-RUN = 4
+RUN = 8
 BLOCK = 16
 TENSOR_COLS = (0, 256, 256, 256)
 VECTOR_COLS = (144, 32, 192, 160)

@@ -25,9 +25,21 @@ BANK_COLS = BANK_TILES * M_TILE
 BANKS = UNIT // BANK_COLS
 RUN = 8
 BLOCK = 16
-TENSOR_COLS = (0, 256, 256, 256)
-VECTOR_COLS = (144, 32, 192, 160)
-QUARTER = SAMPLES * TERMS
+FIRST = (0, 0)
+PIECES = ((UNIT, UNIT), (NODES,))
+BOTH = tuple(range(TERMS))
+FIRST_ROUNDS = (
+    (0, 0, (0,), 0),
+    (0, 0, (1,), 0),
+    (0, 1, BOTH, 0),
+    (0, 0, BOTH, 1),
+    (0, 1, BOTH, 1),
+)
+LAST_ROUNDS = tuple(
+    (LAST, b, (k,), u) for u in range(UNITS) for b in range(SAMPLES) for k in BOTH
+)
+ROUNDS = FIRST_ROUNDS + LAST_ROUNDS
+VECTOR_COLS = (144, 144, 288, 128, 0, 192, 128, 128, 128, 128, 128, 128, 192)
 
 FLOPS = 2 * TERMS * SAMPLES * NODES * NODES * SIGNAL
 
@@ -44,7 +56,8 @@ def tile_napl_conv_withsat_pb_kernel(tc, supports, cheb_2, spatial_attention, x,
     terms = (supports, cheb_2)
     with ExitStack() as ctx:
         keep = ctx.enter_context(tc.tile_pool(name="keep", bufs=1))
-        stage = ctx.enter_context(tc.tile_pool(name="stage", bufs=3))
+        stage = ctx.enter_context(tc.tile_pool(name="stage", bufs=2))
+        stage_grouped = ctx.enter_context(tc.tile_pool(name="stage_grouped", bufs=3))
         psum = ctx.enter_context(tc.psum_pool(name="psum", bufs=4))
         psum_terms = ctx.enter_context(tc.psum_pool(name="psum_terms", bufs=4))
         ctx.enter_context(tc.manual_schedule())
@@ -54,23 +67,23 @@ def tile_napl_conv_withsat_pb_kernel(tc, supports, cheb_2, spatial_attention, x,
         codes = {}
         scales = {}
         att_grouped = {}
-        for c in range(PASSES):
-            for k in range(TERMS):
-                term_sb[k, c] = keep.tile([P, PACK, NODES], BF16, name="term%d_%d" % (k, c))
-            for b in range(SAMPLES):
-                att_sb[b, c] = keep.tile([P, PACK, NODES], BF16, name="att%d_%d" % (b, c))
+        for c, widths in enumerate(PIECES):
+            for i, width in enumerate(widths):
+                name = "%d_%d" % (c, i)
+                term_sb[c, i] = keep.tile([P, TERMS, PACK, width], BF16, name="term" + name)
+                for b in range(SAMPLES):
+                    att_sb[b, c, i] = keep.tile([P, PACK, width], BF16, name="att%d_" % b + name)
+        for s, (c, b, ks, u) in enumerate(ROUNDS):
+            width = len(ks) * UNIT
+            codes[s] = keep.tile([P, width], U32, name="codes%d" % s, align_bytes=64)
+            scales[s] = keep.tile([P, width], U8, name="scales%d" % s, align_bytes=64)
         for b in range(SAMPLES):
-            for k in range(TERMS):
-                codes[b, k] = keep.tile(
-                    [P, PASSES, NODES], U32, name="codes%d_%d" % (b, k), align_bytes=64
-                )
-                scales[b, k] = keep.tile(
-                    [P, PASSES, NODES], U8, name="scales%d_%d" % (b, k), align_bytes=64
-                )
-            for q in range(1, PASSES * UNITS):
-                att_grouped[b, q] = keep.tile(
-                    [P, BANK_COLS, PACK], BF16, name="att_grouped%d_%d" % (b, q)
-                )
+            for c in range(PASSES):
+                for u in range(UNITS):
+                    if (c, u) != FIRST:
+                        att_grouped[b, c, u] = keep.tile(
+                            [P, BANK_COLS, PACK], BF16, name="att_grouped%d_%d_%d" % (b, c, u)
+                        )
         x_sb = keep.tile([P, SAMPLES, PASSES, PACK, SIGNAL], BF16)
         x_grouped = keep.tile([P, SAMPLES, PASSES, SIGNAL, PACK], BF16, align_bytes=64)
         x_codes = keep.tile([P, SAMPLES, PASSES, SIGNAL], U32, align_bytes=64)
@@ -83,7 +96,7 @@ def tile_napl_conv_withsat_pb_kernel(tc, supports, cheb_2, spatial_attention, x,
         def load_columns(slab, matrix, c, cols):
             rows = matrix[c * P * PACK : (c + 1) * P * PACK, :]
             nc.sync.dma_start(
-                out=slab[:, :, cols], in_=rows.rearrange("(p j) m -> p j m", j=PACK)[:, :, cols]
+                out=slab, in_=rows.rearrange("(p j) m -> p j m", j=PACK)[:, :, cols]
             )
 
         for b in range(SAMPLES):
@@ -100,15 +113,20 @@ def tile_napl_conv_withsat_pb_kernel(tc, supports, cheb_2, spatial_attention, x,
                     out=x_sb[:, b, c].rearrange("p j s -> p (j s)"),
                     in_=x[b].rearrange("(c p j) f t -> c p (j f t)", p=P, j=PACK)[c],
                 )
-        for u in range(UNITS):
-            cols = slice(u * UNIT, (u + 1) * UNIT)
-            load_columns(term_sb[0, 0], terms[0], 0, cols)
-            load_columns(att_sb[0, 0], spatial_attention[0], 0, cols)
-            load_columns(term_sb[1, 0], terms[1], 0, cols)
-            load_columns(att_sb[1, 0], spatial_attention[1], 0, cols)
-        for i in range(SAMPLES):
-            load_columns(term_sb[i, LAST], terms[i], LAST, slice(0, NODES))
-            load_columns(att_sb[i, LAST], spatial_attention[i], LAST, slice(0, NODES))
+        for c, widths in enumerate(PIECES):
+            for i, width in enumerate(widths):
+                cols = slice(i * width, (i + 1) * width)
+                for k in range(TERMS):
+                    load_columns(term_sb[c, i][:, k], terms[k], c, cols)
+                    load_columns(att_sb[k, c, i][:], spatial_attention[k], c, cols)
+
+        def term_cols(c, u, first, last):
+            piece, base = (u, 0) if c == 0 else (0, u * UNIT)
+            return term_sb[c, piece][:, :, :, base + first : base + last]
+
+        def att_cols(b, c, u, first, last):
+            piece, base = (u, 0) if c == 0 else (0, u * UNIT)
+            return att_sb[b, c, piece][:, :, base + first : base + last]
 
         for b in range(SAMPLES):
             for c in range(PASSES):
@@ -134,98 +152,122 @@ def tile_napl_conv_withsat_pb_kernel(tc, supports, cheb_2, spatial_attention, x,
                     in_=scaled[:].rearrange("p j s -> p (j s)"),
                 )
 
-        rounds = []
-        for c in range(PASSES):
-            for u in range(UNITS):
-                for b in range(SAMPLES):
-                    for k in range(TERMS):
-                        rounds.append((c, b, k, u))
-
         def tensor_cols(s):
-            return TENSOR_COLS[s // QUARTER]
+            c, b, ks, u = ROUNDS[s]
+            return 0 if (c, u) == FIRST else BANK_COLS
+
+        def first_copied(s):
+            return len(ROUNDS[s][2]) * tensor_cols(s)
 
         term_grouped = {}
 
-        def interleave_term(pool, k, q):
-            c, u = divmod(q, UNITS)
+        def interleave_term(pool, k, c, u):
             bank = pool.tile([P, BANK_COLS, PACK], BF16, name="bank")
             for i in range(BANK_TILES):
-                cols = slice(u * UNIT + i * M_TILE, u * UNIT + (i + 1) * M_TILE)
+                rows = term_cols(c, u, i * M_TILE, (i + 1) * M_TILE)[:, k]
                 nc.tensor.matmul(
                     out=bank[:, i * M_TILE : (i + 1) * M_TILE, :],
                     lhsT=identity[:],
-                    rhs=term_sb[k, c][:, :, cols].rearrange("p j w -> p w j"),
+                    rhs=rows.rearrange("p j w -> p w j"),
                     start=True,
                     stop=True,
                 )
-            term_grouped[k, q] = bank
+            term_grouped[k, c, u] = bank
 
-        def regroup_attention(b, q, i):
-            c, u = divmod(q, UNITS)
-            regroup(
-                nc.scalar.copy,
-                att_grouped[b, q][:, i * M_TILE : (i + 1) * M_TILE, :],
-                att_sb[b, c][:, :, u * UNIT + i * M_TILE : u * UNIT + (i + 1) * M_TILE],
-            )
+        def regroup_attention(b, c, u):
+            regroup(nc.scalar.copy, att_grouped[b, c, u][:], att_cols(b, c, u, 0, BANK_COLS))
 
         def multiply(s):
-            c, b, k, u = rounds[s]
-            cols = slice(u * UNIT + tensor_cols(s), (u + 1) * UNIT)
-            product = stage.tile([P, PACK, UNIT], BF16, name="product")
-            nc.vector.tensor_tensor(
-                out=product[:, :, tensor_cols(s) :],
-                in0=term_sb[k, c][:, :, cols],
-                in1=att_sb[b, c][:, :, cols],
-                op=mybir.AluOpType.mult,
-            )
-            return product
-
-        def group(s, product, vector_cols):
-            c, b, k, u = rounds[s]
-            grouped = stage.tile([P, UNIT, PACK], BF16, align_bytes=64, name="grouped")
-            if tensor_cols(s):
+            c, b, ks, u = ROUNDS[s]
+            width = UNIT - tensor_cols(s)
+            product = stage.tile([P, PACK, len(ks) * width], BF16, name="product")
+            term = term_cols(c, u, tensor_cols(s), UNIT)
+            att = att_cols(b, c, u, tensor_cols(s), UNIT)
+            if len(ks) == 1:
                 nc.vector.tensor_tensor(
-                    out=grouped[:, : tensor_cols(s), :],
-                    in0=term_grouped[k, s // QUARTER][:],
-                    in1=att_grouped[b, s // QUARTER][:],
+                    out=product[:],
+                    in0=term[:, ks[0]],
+                    in1=att,
                     op=mybir.AluOpType.mult,
                 )
-            split = tensor_cols(s) + vector_cols
-            if split > tensor_cols(s):
-                regroup(
-                    nc.vector.tensor_copy,
-                    grouped[:, tensor_cols(s) : split, :],
-                    product[:, :, tensor_cols(s) : split],
+            else:
+                nc.vector.tensor_tensor(
+                    out=product[:].rearrange("p j (k w) -> p k j w", k=TERMS),
+                    in0=term,
+                    in1=att.unsqueeze(1).to_broadcast([P, TERMS, PACK, width]),
+                    op=mybir.AluOpType.mult,
                 )
-            if split < UNIT:
-                regroup(nc.scalar.copy, grouped[:, split:, :], product[:, :, split:])
+            return product
+
+        def open_group(s):
+            c, b, ks, u = ROUNDS[s]
+            grouped = stage_grouped.tile(
+                [P, len(ks) * UNIT, PACK], BF16, align_bytes=64, name="grouped"
+            )
+            if first_copied(s):
+                for i, k in enumerate(ks):
+                    nc.vector.tensor_tensor(
+                        out=grouped[:, i * BANK_COLS : (i + 1) * BANK_COLS, :],
+                        in0=term_grouped[k, c, u][:],
+                        in1=att_grouped[b, c, u][:],
+                        op=mybir.AluOpType.mult,
+                    )
             return grouped
 
-        def quantise(c, b, k, first, grouped):
-            cols = slice(first, first + grouped.shape[1])
+        def vector_group(s):
+            base, split = first_copied(s), VECTOR_COLS[s]
+            if split:
+                regroup(
+                    nc.vector.tensor_copy,
+                    groupeds[s][:, base : base + split, :],
+                    products[s][:, :, :split],
+                )
+
+        def scalar_group(s):
+            base, split = first_copied(s), VECTOR_COLS[s]
+            if base + split == groupeds[s].shape[1]:
+                return
+            regroup(nc.scalar.copy, groupeds[s][:, base + split :, :], products[s][:, :, split:])
+
+        def quantise(s, first, last):
             nc.vector.quantize_mx(
-                out=codes[b, k][:, c, cols].bitcast(FP8X4),
-                scales=scales[b, k][:, c, cols],
-                in_=grouped.rearrange("p w j -> p (w j)"),
+                out=codes[s][:, first:last].bitcast(FP8X4),
+                scales=scales[s][:, first:last],
+                in_=groupeds[s][:, first:last, :].rearrange("p w j -> p (w j)"),
             )
 
-        def add_pass(sums_of_tile, b, k, c, first):
-            m_cols = slice(first, first + M_TILE)
+        round_of = {}
+        for s, (c, b, ks, u) in enumerate(ROUNDS):
+            for k in ks:
+                round_of[c, b, k, u] = s
+
+        def code_cols(s, k, i):
+            j = ROUNDS[s][2].index(k)
+            first = i * M_TILE
+            if first < tensor_cols(s):
+                first += j * tensor_cols(s)
+            else:
+                first += first_copied(s) + j * (UNIT - tensor_cols(s)) - tensor_cols(s)
+            return slice(first, first + M_TILE)
+
+        def add_pass(sums_of_tile, b, k, u, c, i):
+            s = round_of[c, b, k, u]
+            cols = code_cols(s, k, i)
             nc.tensor.matmul_mx(
                 out=sums_of_tile,
-                lhsT=codes[b, k][:, c, m_cols].bitcast(FP8X4),
-                lhsT_scale=scales[b, k][:, c, m_cols],
+                lhsT=codes[s][:, cols].bitcast(FP8X4),
+                lhsT_scale=scales[s][:, cols],
                 rhs=x_codes[:, b, c, :].bitcast(FP8X4),
                 rhs_scale=x_scales[:, b, c, :],
                 start=(c == 0),
                 stop=(c == LAST),
             )
 
-        def contract(b, k, first):
+        def contract(b, k, u, half):
             acc = psum.tile([P, BANK_TILES, SIGNAL], F32, name="bank")
             for i in range(BANK_TILES):
                 for c in range(PASSES):
-                    add_pass(acc[:, i, :], b, k, c, first + i * M_TILE)
+                    add_pass(acc[:, i, :], b, k, u, c, half * BANK_TILES + i)
             return acc
 
         def empty_and_store(engine_copy, b, k, first, acc):
@@ -235,73 +277,79 @@ def tile_napl_conv_withsat_pb_kernel(tc, supports, cheb_2, spatial_attention, x,
             rows = out[1 + k, b, first : first + tiles * M_TILE]
             nc.sync.dma_start(out=rows.rearrange("(t p) f s -> p t (f s)", p=P), in_=result[:])
 
-        attention_jobs = {}
-        for q in range(1, PASSES * UNITS):
-            for b in range(SAMPLES):
-                for i in range(BANK_TILES):
-                    attention_jobs[QUARTER * q + TERMS * b - BANK_TILES + i] = (b, q, i)
+        attention_jobs = {
+            2: [(0, 0, 1)],
+            3: [(1, 0, 1)],
+            4: [(0, LAST, 0)],
+            5: [(1, LAST, 0)],
+            7: [(0, LAST, 1)],
+            9: [(1, LAST, 1)],
+        }
         term_jobs = {
-            1: [(psum, 0, 1), (psum, 1, 1)],
-            QUARTER: [(psum_terms, 0, 2), (psum_terms, 0, 3), (psum_terms, 1, 2), (psum_terms, 1, 3)],
+            1: [(psum, k, 0, 1) for k in BOTH],
+            3: [(psum_terms, k, LAST, u) for k in BOTH for u in range(UNITS)],
         }
 
         def quantise_and_contract(s):
-            c, b, k, u = rounds[s]
+            c, b, ks, u = ROUNDS[s]
+            quantise(s, 0, len(ks) * UNIT)
             if c < LAST:
-                quantise(c, b, k, u * UNIT, groupeds[s][:])
                 return []
-            banks = []
-            for i in range(BANKS):
-                first = u * UNIT + i * BANK_COLS
-                quantise(c, b, k, first, groupeds[s][:, i * BANK_COLS : (i + 1) * BANK_COLS, :])
-                banks.append(contract(b, k, first))
-            return banks
+            return [(k, half, contract(b, k, u, half)) for k in ks for half in range(BANKS)]
 
         def empty_round(s, engine_copies):
-            c, b, k, u = rounds[s]
-            for i in range(len(sums[s])):
-                empty_and_store(engine_copies[i], b, k, u * UNIT + i * BANK_COLS, sums[s][i][:])
+            c, b, ks, u = ROUNDS[s]
+            for i, (k, half, acc) in enumerate(sums[s]):
+                empty_and_store(
+                    engine_copies[i % len(engine_copies)], b, k, u * UNIT + half * BANK_COLS, acc[:]
+                )
 
-        final = len(rounds) - 1
+        final = len(ROUNDS) - 1
         products = {0: multiply(0)}
         groupeds = {}
         sums = {}
         for s in range(final - 1):
-            if s in attention_jobs:
-                regroup_attention(*attention_jobs[s])
-            groupeds[s] = group(s, products[s], VECTOR_COLS[s // QUARTER])
+            for job in attention_jobs.get(s, []):
+                regroup_attention(*job)
+            groupeds[s] = open_group(s)
+            vector_group(s)
+            scalar_group(s)
             products[s + 1] = multiply(s + 1)
             if s >= 1:
                 sums[s - 1] = quantise_and_contract(s - 1)
-            for pool, k, q in term_jobs.get(s, []):
-                interleave_term(pool, k, q)
+            for job in term_jobs.get(s, []):
+                interleave_term(*job)
             if s >= 2:
-                empty_round(s - 2, (nc.scalar.copy, nc.scalar.copy))
+                empty_round(s - 2, (nc.scalar.copy,))
 
-        groupeds[final - 1] = group(final - 1, products[final - 1], VECTOR_COLS[-1])
+        c, b, ks, u = ROUNDS[final]
+        k = ks[0]
+        tiles = UNIT // M_TILE
+        groupeds[final - 1] = open_group(final - 1)
+        vector_group(final - 1)
+        scalar_group(final - 1)
         sums[final - 2] = quantise_and_contract(final - 2)
         products[final] = multiply(final)
-        empty_round(final - 3, (nc.scalar.copy, nc.scalar.copy))
-        c, b, k, u = rounds[final]
-        tiles = UNIT // M_TILE
+        empty_round(final - 3, (nc.scalar.copy,))
         final_sums = []
 
         def open_final_sum():
             i = len(final_sums)
             final_sums.append(psum_terms.tile([P, BANK_TILES, SIGNAL], F32, name="bank"))
-            add_pass(final_sums[i][:, 0, :], b, k, 0, u * UNIT + i * M_TILE)
+            add_pass(final_sums[i][:, 0, :], b, k, u, 0, i)
 
         for i in range(tiles - 1):
             open_final_sum()
         sums[final - 1] = quantise_and_contract(final - 1)
-        groupeds[final] = group(final, products[final], UNIT - tensor_cols(final))
+        groupeds[final] = open_group(final)
+        vector_group(final)
+        scalar_group(final)
         open_final_sum()
-        empty_round(final - 2, (nc.scalar.copy, nc.scalar.copy))
-        for i in range(BANKS):
-            first = u * UNIT + i * BANK_COLS
-            quantise(c, b, k, first, groupeds[final][:, i * BANK_COLS : (i + 1) * BANK_COLS, :])
-            for t in range(i * BANK_TILES, (i + 1) * BANK_TILES):
-                add_pass(final_sums[t][:, 0, :], b, k, LAST, u * UNIT + t * M_TILE)
+        empty_round(final - 2, (nc.scalar.copy,))
+        for half in range(BANKS):
+            quantise(final, half * BANK_COLS, (half + 1) * BANK_COLS)
+            for i in range(half * BANK_TILES, (half + 1) * BANK_TILES):
+                add_pass(final_sums[i][:, 0, :], b, k, u, LAST, i)
         empty_round(final - 1, (nc.scalar.copy, nc.vector.tensor_copy))
         for i in range(tiles):
             empty_and_store(

@@ -27,6 +27,7 @@ RUN = 8
 BLOCK = 16
 FIRST = (0, 0)
 PIECES = ((UNIT, UNIT), (NODES,))
+FIRST_ROWS = PACK // 2
 BOTH = tuple(range(TERMS))
 FIRST_ROUNDS = (
     (0, 0, (0,), 0),
@@ -93,12 +94,6 @@ def tile_napl_conv_withsat_pb_kernel(tc, supports, cheb_2, spatial_attention, x,
         identity = keep.tile([P, P], BF16)
         masks.make_identity(nc, identity[:])
 
-        def load_columns(slab, matrix, c, cols):
-            rows = matrix[c * P * PACK : (c + 1) * P * PACK, :]
-            nc.sync.dma_start(
-                out=slab, in_=rows.rearrange("(p j) m -> p j m", j=PACK)[:, :, cols]
-            )
-
         for b in range(SAMPLES):
             flat = spatial_attention[b].rearrange("n m -> (n m)")
             on_diagonal = flat[0 : NODES * NODES : NODES + 1]
@@ -113,12 +108,26 @@ def tile_napl_conv_withsat_pb_kernel(tc, supports, cheb_2, spatial_attention, x,
                     out=x_sb[:, b, c].rearrange("p j s -> p (j s)"),
                     in_=x[b].rearrange("(c p j) f t -> c p (j f t)", p=P, j=PACK)[c],
                 )
+        def load_piece(c, i, m, first, last):
+            width = PIECES[c][i]
+            cols = slice(i * width, (i + 1) * width)
+            for slab, matrix in (
+                (term_sb[c, i][:, m], terms[m]),
+                (att_sb[m, c, i][:], spatial_attention[m]),
+            ):
+                rows = matrix[c * P * PACK : (c + 1) * P * PACK, cols]
+                nc.sync.dma_start(
+                    out=slab[:, first:last, :],
+                    in_=rows.rearrange("(p j) m -> p j m", j=PACK)[:, first:last, :],
+                )
+
+        for first in range(0, PACK, FIRST_ROWS):
+            load_piece(0, 0, 0, first, first + FIRST_ROWS)
         for c, widths in enumerate(PIECES):
-            for i, width in enumerate(widths):
-                cols = slice(i * width, (i + 1) * width)
-                for k in range(TERMS):
-                    load_columns(term_sb[c, i][:, k], terms[k], c, cols)
-                    load_columns(att_sb[k, c, i][:], spatial_attention[k], c, cols)
+            for i in range(len(widths)):
+                for m in range(TERMS):
+                    if (c, i, m) != (0, 0, 0):
+                        load_piece(c, i, m, 0, PACK)
 
         def term_cols(c, u, first, last):
             piece, base = (u, 0) if c == 0 else (0, u * UNIT)
@@ -184,12 +193,14 @@ def tile_napl_conv_withsat_pb_kernel(tc, supports, cheb_2, spatial_attention, x,
             term = term_cols(c, u, tensor_cols(s), UNIT)
             att = att_cols(b, c, u, tensor_cols(s), UNIT)
             if len(ks) == 1:
-                nc.vector.tensor_tensor(
-                    out=product[:],
-                    in0=term[:, ks[0]],
-                    in1=att,
-                    op=mybir.AluOpType.mult,
-                )
+                rows = FIRST_ROWS if s == 0 else PACK
+                for first in range(0, PACK, rows):
+                    nc.vector.tensor_tensor(
+                        out=product[:, first : first + rows, :],
+                        in0=term[:, ks[0], first : first + rows, :],
+                        in1=att[:, first : first + rows, :],
+                        op=mybir.AluOpType.mult,
+                    )
             else:
                 nc.vector.tensor_tensor(
                     out=product[:].rearrange("p j (k w) -> p k j w", k=TERMS),

@@ -37,10 +37,11 @@ FIRST_ROUNDS = (
     (0, 1, BOTH, 1),
 )
 LAST_ROUNDS = tuple(
-    (LAST, b, (k,), u) for u in range(UNITS) for b in range(SAMPLES) for k in BOTH
+    (LAST, b, (k,), u) for u in range(UNITS) for k in BOTH for b in range(SAMPLES)
 )
 ROUNDS = FIRST_ROUNDS + LAST_ROUNDS
-VECTOR_COLS = (144, 144, 288, 128, 0, 192, 128, 128, 128, 128, 128, 128, 192)
+VECTOR_COLS = (160, 160, 320, 128, 0)
+VECTOR_ATT_COLS = ((512, 128), (0, 128))
 
 FLOPS = 2 * TERMS * SAMPLES * NODES * NODES * SIGNAL
 
@@ -52,18 +53,27 @@ def regroup(engine_copy, grouped, rows):
     )
 
 
+def tensor_width(c, u):
+    if c == LAST:
+        return UNIT
+    return 0 if (c, u) == FIRST else BANK_COLS
+
+
 def tile_napl_conv_withsat_pb_kernel(tc, supports, cheb_2, spatial_attention, x, out):
     nc = tc.nc
     terms = (supports, cheb_2)
     with ExitStack() as ctx:
         keep = ctx.enter_context(tc.tile_pool(name="keep", bufs=1))
         stage = ctx.enter_context(tc.tile_pool(name="stage", bufs=2))
-        stage_grouped = ctx.enter_context(tc.tile_pool(name="stage_grouped", bufs=3))
+        stage_first = ctx.enter_context(tc.tile_pool(name="stage_first", bufs=3))
+        stage_last = ctx.enter_context(tc.tile_pool(name="stage_last", bufs=2))
+        results = ctx.enter_context(tc.tile_pool(name="results", bufs=6))
         psum = ctx.enter_context(tc.psum_pool(name="psum", bufs=4))
         psum_terms = ctx.enter_context(tc.psum_pool(name="psum_terms", bufs=4))
         ctx.enter_context(tc.manual_schedule())
 
         term_sb = {}
+        term_turned = {}
         att_sb = {}
         codes = {}
         scales = {}
@@ -71,9 +81,12 @@ def tile_napl_conv_withsat_pb_kernel(tc, supports, cheb_2, spatial_attention, x,
         for c, widths in enumerate(PIECES):
             for i, width in enumerate(widths):
                 name = "%d_%d" % (c, i)
-                term_sb[c, i] = keep.tile([P, TERMS, PACK, width], BF16, name="term" + name)
+                term_sb[c, i] = keep.tile([P, TERMS, PACK, UNIT], BF16, name="term" + name)
                 for b in range(SAMPLES):
                     att_sb[b, c, i] = keep.tile([P, PACK, width], BF16, name="att%d_" % b + name)
+        term_rows = keep.tile([P, TERMS, PACK, UNIT], BF16)
+        for k in range(TERMS):
+            term_turned[k] = keep.tile([P, UNIT // P, PACK * P], BF16, name="term_turned%d" % k)
         for s, (c, b, ks, u) in enumerate(ROUNDS):
             width = len(ks) * UNIT
             codes[s] = keep.tile([P, width], U32, name="codes%d" % s, align_bytes=64)
@@ -83,7 +96,7 @@ def tile_napl_conv_withsat_pb_kernel(tc, supports, cheb_2, spatial_attention, x,
                 for u in range(UNITS):
                     if (c, u) != FIRST:
                         att_grouped[b, c, u] = keep.tile(
-                            [P, BANK_COLS, PACK], BF16, name="att_grouped%d_%d_%d" % (b, c, u)
+                            [P, tensor_width(c, u), PACK], BF16, name="att_grouped%d_%d_%d" % (b, c, u)
                         )
         x_sb = keep.tile([P, SAMPLES, PASSES, PACK, SIGNAL], BF16)
         x_grouped = keep.tile([P, SAMPLES, PASSES, SIGNAL, PACK], BF16, align_bytes=64)
@@ -93,6 +106,8 @@ def tile_napl_conv_withsat_pb_kernel(tc, supports, cheb_2, spatial_attention, x,
         diag = keep.tile([P, SAMPLES, PASSES, PACK], F32)
         identity = keep.tile([P, P], BF16)
         masks.make_identity(nc, identity[:])
+        identity_f32 = keep.tile([P, P], F32)
+        masks.make_identity(nc, identity_f32[:])
 
         for b in range(SAMPLES):
             flat = spatial_attention[b].rearrange("n m -> (n m)")
@@ -108,30 +123,29 @@ def tile_napl_conv_withsat_pb_kernel(tc, supports, cheb_2, spatial_attention, x,
                     out=x_sb[:, b, c].rearrange("p j s -> p (j s)"),
                     in_=x[b].rearrange("(c p j) f t -> c p (j f t)", p=P, j=PACK)[c],
                 )
-        def load_piece(c, i, m, first, last):
-            width = PIECES[c][i]
-            cols = slice(i * width, (i + 1) * width)
-            for slab, matrix in (
-                (term_sb[c, i][:, m], terms[m]),
-                (att_sb[m, c, i][:], spatial_attention[m]),
-            ):
-                rows = matrix[c * P * PACK : (c + 1) * P * PACK, cols]
-                nc.sync.dma_start(
-                    out=slab[:, first:last, :],
-                    in_=rows.rearrange("(p j) m -> p j m", j=PACK)[:, first:last, :],
-                )
+        def load_rows(slab, matrix, c, cols, first=0, last=PACK):
+            rows = matrix[c * P * PACK : (c + 1) * P * PACK, cols]
+            nc.sync.dma_start(
+                out=slab[:, first:last, :],
+                in_=rows.rearrange("(p j) m -> p j m", j=PACK)[:, first:last, :],
+            )
 
         for first in range(0, PACK, FIRST_ROWS):
-            load_piece(0, 0, 0, first, first + FIRST_ROWS)
-        for c, widths in enumerate(PIECES):
-            for i in range(len(widths)):
-                for m in range(TERMS):
-                    if (c, i, m) != (0, 0, 0):
-                        load_piece(c, i, m, 0, PACK)
-
-        def term_cols(c, u, first, last):
-            piece, base = (u, 0) if c == 0 else (0, u * UNIT)
-            return term_sb[c, piece][:, :, :, base + first : base + last]
+            for slab, matrix in ((term_sb[0, 0][:, 0], terms[0]), (att_sb[0, 0, 0][:], spatial_attention[0])):
+                load_rows(slab, matrix, 0, slice(0, UNIT), first, first + FIRST_ROWS)
+        for i in range(UNITS):
+            cols = slice(i * UNIT, (i + 1) * UNIT)
+            for m in range(TERMS):
+                if (i, m) != (0, 0):
+                    load_rows(term_sb[0, i][:, m], terms[m], 0, cols)
+                    load_rows(att_sb[m, 0, i][:], spatial_attention[m], 0, cols)
+        load_rows(att_sb[0, LAST, 0][:], spatial_attention[0], LAST, slice(0, NODES))
+        for k in range(TERMS):
+            load_rows(term_sb[LAST, 0][:, k], terms[k], LAST, slice(0, UNIT))
+        load_rows(att_sb[1, LAST, 0][:], spatial_attention[1], LAST, slice(0, NODES))
+        for k in range(TERMS):
+            rows = terms[k][LAST * P * PACK : (LAST + 1) * P * PACK, UNIT:]
+            nc.sync.dma_start(out=term_rows[:, k], in_=rows.rearrange("(t p) m -> p t m", p=P))
 
         def att_cols(b, c, u, first, last):
             piece, base = (u, 0) if c == 0 else (0, u * UNIT)
@@ -163,34 +177,77 @@ def tile_napl_conv_withsat_pb_kernel(tc, supports, cheb_2, spatial_attention, x,
 
         def tensor_cols(s):
             c, b, ks, u = ROUNDS[s]
-            return 0 if (c, u) == FIRST else BANK_COLS
+            return tensor_width(c, u)
 
         def first_copied(s):
             return len(ROUNDS[s][2]) * tensor_cols(s)
 
         term_grouped = {}
 
-        def interleave_term(pool, k, c, u):
+        def interleave_term(pool, k, c, u, half):
+            piece = u if c == 0 else 0
             bank = pool.tile([P, BANK_COLS, PACK], BF16, name="bank")
             for i in range(BANK_TILES):
-                rows = term_cols(c, u, i * M_TILE, (i + 1) * M_TILE)[:, k]
+                first = half * BANK_COLS + i * M_TILE
                 nc.tensor.matmul(
                     out=bank[:, i * M_TILE : (i + 1) * M_TILE, :],
                     lhsT=identity[:],
-                    rhs=rows.rearrange("p j w -> p w j"),
+                    rhs=term_sb[c, piece][:, k, :, first : first + M_TILE].rearrange("p j w -> p w j"),
                     start=True,
                     stop=True,
                 )
-            term_grouped[k, c, u] = bank
+            term_grouped[k, c, u, half] = bank
+
+        def turn_term(k, half):
+            bank = psum.tile([P, BANK_TILES, PACK * P], BF16, name="bank")
+            for i in range(BANK_TILES):
+                first = half * BANK_COLS + i * M_TILE
+                for t in range(PACK):
+                    nc.tensor.transpose(
+                        bank[:, i, t * P : (t + 1) * P],
+                        term_rows[:, k, t, first : first + M_TILE],
+                        identity[:],
+                    )
+            turned_banks[k, half] = bank
+
+        def keep_turned_term(k, half):
+            tiles = slice(half * BANK_TILES, (half + 1) * BANK_TILES)
+            nc.scalar.copy(out=term_turned[k][:, tiles, :], in_=turned_banks[k, half][:])
+
+        def turn_term_back(k, half):
+            bank = psum_terms.tile([P, BANK_COLS, PACK], BF16, name="bank")
+            words = bank[:].bitcast(F32)
+            turned = term_turned[k][:].bitcast(F32)
+            for i in range(BANK_TILES):
+                for r in range(PACK // 2):
+                    nc.tensor.transpose(
+                        words[:, i * M_TILE : (i + 1) * M_TILE, r],
+                        turned[:, half * BANK_TILES + i, r : PACK * P // 2 : 2],
+                        identity_f32[:],
+                    )
+            term_grouped[k, LAST, UNITS - 1, half] = bank
+
+        def fill_banks(k, u):
+            for half in range(BANKS):
+                if u < UNITS - 1:
+                    interleave_term(psum_terms, k, LAST, u, half)
+                else:
+                    turn_term_back(k, half)
 
         def regroup_attention(b, c, u):
-            regroup(nc.scalar.copy, att_grouped[b, c, u][:], att_cols(b, c, u, 0, BANK_COLS))
+            width = tensor_width(c, u)
+            grouped, rows = att_grouped[b, c, u], att_cols(b, c, u, 0, width)
+            split = VECTOR_ATT_COLS[b][u] if c == LAST else 0
+            if split:
+                regroup(nc.vector.tensor_copy, grouped[:, :split, :], rows[:, :, :split])
+            if split < width:
+                regroup(nc.scalar.copy, grouped[:, split:, :], rows[:, :, split:])
 
         def multiply(s):
             c, b, ks, u = ROUNDS[s]
             width = UNIT - tensor_cols(s)
             product = stage.tile([P, PACK, len(ks) * width], BF16, name="product")
-            term = term_cols(c, u, tensor_cols(s), UNIT)
+            term = term_sb[c, u][:, :, :, tensor_cols(s) :]
             att = att_cols(b, c, u, tensor_cols(s), UNIT)
             if len(ks) == 1:
                 rows = FIRST_ROWS if s == 0 else PACK
@@ -212,18 +269,19 @@ def tile_napl_conv_withsat_pb_kernel(tc, supports, cheb_2, spatial_attention, x,
 
         def open_group(s):
             c, b, ks, u = ROUNDS[s]
-            grouped = stage_grouped.tile(
-                [P, len(ks) * UNIT, PACK], BF16, align_bytes=64, name="grouped"
-            )
-            if first_copied(s):
-                for i, k in enumerate(ks):
-                    nc.vector.tensor_tensor(
-                        out=grouped[:, i * BANK_COLS : (i + 1) * BANK_COLS, :],
-                        in0=term_grouped[k, c, u][:],
-                        in1=att_grouped[b, c, u][:],
-                        op=mybir.AluOpType.mult,
-                    )
+            pool = stage_first if c == 0 else stage_last
+            grouped = pool.tile([P, len(ks) * UNIT, PACK], BF16, align_bytes=64, name="grouped")
             return grouped
+
+        def multiply_bank(s, k, half):
+            c, b, ks, u = ROUNDS[s]
+            first = ks.index(k) * tensor_cols(s) + half * BANK_COLS
+            nc.vector.tensor_tensor(
+                out=groupeds[s][:, first : first + BANK_COLS, :],
+                in0=term_grouped[k, c, u, half][:],
+                in1=att_grouped[b, c, u][:, half * BANK_COLS : (half + 1) * BANK_COLS, :],
+                op=mybir.AluOpType.mult,
+            )
 
         def vector_group(s):
             base, split = first_copied(s), VECTOR_COLS[s]
@@ -283,23 +341,10 @@ def tile_napl_conv_withsat_pb_kernel(tc, supports, cheb_2, spatial_attention, x,
 
         def empty_and_store(engine_copy, b, k, first, acc):
             tiles = acc.shape[1]
-            result = keep.tile([P, tiles, SIGNAL], F32, name="result%d_%d_%d" % (b, k, first))
+            result = results.tile([P, tiles, SIGNAL], F32, name="result")
             engine_copy(out=result[:], in_=acc)
             rows = out[1 + k, b, first : first + tiles * M_TILE]
             nc.sync.dma_start(out=rows.rearrange("(t p) f s -> p t (f s)", p=P), in_=result[:])
-
-        attention_jobs = {
-            2: [(0, 0, 1)],
-            3: [(1, 0, 1)],
-            4: [(0, LAST, 0)],
-            5: [(1, LAST, 0)],
-            7: [(0, LAST, 1)],
-            9: [(1, LAST, 1)],
-        }
-        term_jobs = {
-            1: [(psum, k, 0, 1) for k in BOTH],
-            3: [(psum_terms, k, LAST, u) for k in BOTH for u in range(UNITS)],
-        }
 
         def quantise_and_contract(s):
             c, b, ks, u = ROUNDS[s]
@@ -315,58 +360,72 @@ def tile_napl_conv_withsat_pb_kernel(tc, supports, cheb_2, spatial_attention, x,
                     engine_copies[i % len(engine_copies)], b, k, u * UNIT + half * BANK_COLS, acc[:]
                 )
 
+        attention_jobs = {2: [(0, 0, 1)], 3: [(1, 0, 1)]}
+        late_attention_jobs = {
+            4: [(0, LAST, 0), (1, LAST, 0)],
+            7: [(0, LAST, 1)],
+            8: [(1, LAST, 1)],
+        }
+        bank_jobs = {3: (0, 0), 4: (1, 0), 7: (0, 1), 9: (1, 1)}
+        turn_jobs = {4: [(0, 0), (0, 1)], 5: [(1, 0), (1, 1)]}
+        turned_banks = {}
+
         final = len(ROUNDS) - 1
         products = {0: multiply(0)}
         groupeds = {}
         sums = {}
-        for s in range(final - 1):
+        for s in range(final):
             for job in attention_jobs.get(s, []):
                 regroup_attention(*job)
+            for job in turn_jobs.get(s - 1, []):
+                keep_turned_term(*job)
             groupeds[s] = open_group(s)
-            vector_group(s)
-            scalar_group(s)
-            products[s + 1] = multiply(s + 1)
+            c, b, ks, u = ROUNDS[s]
+            if tensor_cols(s):
+                for k in ks:
+                    multiply_bank(s, k, 0)
+            if c == 0:
+                vector_group(s)
+                scalar_group(s)
+            if s + 1 < len(FIRST_ROUNDS):
+                products[s + 1] = multiply(s + 1)
+            if s == final - 1:
+                final_sums = []
+                for i in range(BANK_TILES):
+                    final_sums.append(psum_terms.tile([P, BANK_TILES, SIGNAL], F32, name="bank"))
+                    add_pass(final_sums[i][:, 0, :], SAMPLES - 1, TERMS - 1, UNITS - 1, 0, BANK_TILES + i)
             if s >= 1:
                 sums[s - 1] = quantise_and_contract(s - 1)
-            for job in term_jobs.get(s, []):
-                interleave_term(*job)
+            if c == LAST:
+                multiply_bank(s, ks[0], 1)
+            for job in late_attention_jobs.get(s, []):
+                regroup_attention(*job)
+            if s == 1:
+                for k in BOTH:
+                    interleave_term(psum, k, 0, 1, 0)
+            if s in bank_jobs:
+                fill_banks(*bank_jobs[s])
+            for job in turn_jobs.get(s, []):
+                turn_term(*job)
             if s >= 2:
                 empty_round(s - 2, (nc.scalar.copy,))
 
         c, b, ks, u = ROUNDS[final]
         k = ks[0]
-        tiles = UNIT // M_TILE
-        groupeds[final - 1] = open_group(final - 1)
-        vector_group(final - 1)
-        scalar_group(final - 1)
-        sums[final - 2] = quantise_and_contract(final - 2)
-        products[final] = multiply(final)
-        empty_round(final - 3, (nc.scalar.copy,))
-        final_sums = []
-
-        def open_final_sum():
-            i = len(final_sums)
-            final_sums.append(psum_terms.tile([P, BANK_TILES, SIGNAL], F32, name="bank"))
-            add_pass(final_sums[i][:, 0, :], b, k, u, 0, i)
-
-        for i in range(tiles - 1):
-            open_final_sum()
-        sums[final - 1] = quantise_and_contract(final - 1)
         groupeds[final] = open_group(final)
-        vector_group(final)
-        scalar_group(final)
-        open_final_sum()
+        multiply_bank(final, k, 0)
+        sums[final - 1] = quantise_and_contract(final - 1)
+        multiply_bank(final, k, 1)
         empty_round(final - 2, (nc.scalar.copy,))
         for half in range(BANKS):
             quantise(final, half * BANK_COLS, (half + 1) * BANK_COLS)
-            for i in range(half * BANK_TILES, (half + 1) * BANK_TILES):
-                add_pass(final_sums[i][:, 0, :], b, k, u, LAST, i)
-        empty_round(final - 1, (nc.scalar.copy, nc.vector.tensor_copy))
-        for i in range(tiles):
-            empty_and_store(
-                (nc.scalar.copy, nc.vector.tensor_copy)[i % 2],
-                b,
-                k,
-                u * UNIT + i * M_TILE,
-                final_sums[i][:, :1, :],
-            )
+            if half == 0:
+                first_sums = contract(b, k, u, half)
+            else:
+                for i in range(BANK_TILES):
+                    add_pass(final_sums[i][:, 0, :], b, k, u, LAST, BANK_TILES + i)
+        empty_round(final - 1, (nc.scalar.copy,))
+        empty_and_store(nc.vector.tensor_copy, b, k, u * UNIT, first_sums[:])
+        for i, engine_copy in enumerate((nc.scalar.copy, nc.vector.tensor_copy)):
+            first = u * UNIT + BANK_COLS + i * M_TILE
+            empty_and_store(engine_copy, b, k, first, final_sums[i][:, :1, :])

@@ -133,12 +133,14 @@ def tile_napl_conv_withsat_pb_kernel(tc, supports, cheb_2, spatial_attention, x,
         for first in range(0, PACK, FIRST_ROWS):
             for slab, matrix in ((term_sb[0, 0][:, 0], terms[0]), (att_sb[0, 0, 0][:], spatial_attention[0])):
                 load_rows(slab, matrix, 0, slice(0, UNIT), first, first + FIRST_ROWS)
-        for i in range(UNITS):
-            cols = slice(i * UNIT, (i + 1) * UNIT)
-            for m in range(TERMS):
-                if (i, m) != (0, 0):
-                    load_rows(term_sb[0, i][:, m], terms[m], 0, cols)
-                    load_rows(att_sb[m, 0, i][:], spatial_attention[m], 0, cols)
+        cols = slice(0, UNIT)
+        load_rows(term_sb[0, 0][:, 1], terms[1], 0, cols)
+        load_rows(att_sb[1, 0, 0][:], spatial_attention[1], 0, cols)
+        cols = slice(UNIT, NODES)
+        load_rows(att_sb[0, 0, 1][:], spatial_attention[0], 0, cols)
+        for k in range(TERMS):
+            load_rows(term_sb[0, 1][:, k], terms[k], 0, cols)
+        load_rows(att_sb[1, 0, 1][:], spatial_attention[1], 0, cols)
         load_rows(att_sb[0, LAST, 0][:], spatial_attention[0], LAST, slice(0, NODES))
         for k in range(TERMS):
             load_rows(term_sb[LAST, 0][:, k], terms[k], LAST, slice(0, UNIT))
@@ -190,9 +192,9 @@ def tile_napl_conv_withsat_pb_kernel(tc, supports, cheb_2, spatial_attention, x,
             for i in range(BANK_TILES):
                 first = half * BANK_COLS + i * M_TILE
                 nc.tensor.matmul(
-                    out=bank[:, i * M_TILE : (i + 1) * M_TILE, :],
+                    out=bank[:, i * M_TILE : (i + 1) * M_TILE, :].rearrange("p w j -> p j w"),
                     lhsT=identity[:],
-                    rhs=term_sb[c, piece][:, k, :, first : first + M_TILE].rearrange("p j w -> p w j"),
+                    rhs=term_sb[c, piece][:, k, :, first : first + M_TILE],
                     start=True,
                     stop=True,
                 )

@@ -40,8 +40,8 @@ LAST_ROUNDS = tuple(
     (LAST, b, (k,), u) for u in range(UNITS) for k in BOTH for b in range(SAMPLES)
 )
 ROUNDS = FIRST_ROUNDS + LAST_ROUNDS
-VECTOR_COLS = (160, 160, 320, 128, 0)
-VECTOR_ATT_COLS = ((512, 128), (0, 128))
+VECTOR_COLS = (144, 144, 288, 128, 0)
+VECTOR_ATT_COLS = ((512, 256), (0, 128))
 
 FLOPS = 2 * TERMS * SAMPLES * NODES * NODES * SIGNAL
 
@@ -67,7 +67,7 @@ def tile_napl_conv_withsat_pb_kernel(tc, supports, cheb_2, spatial_attention, x,
         stage = ctx.enter_context(tc.tile_pool(name="stage", bufs=2))
         stage_first = ctx.enter_context(tc.tile_pool(name="stage_first", bufs=3))
         stage_last = ctx.enter_context(tc.tile_pool(name="stage_last", bufs=2))
-        results = ctx.enter_context(tc.tile_pool(name="results", bufs=6))
+        results = ctx.enter_context(tc.tile_pool(name="results", bufs=8))
         psum = ctx.enter_context(tc.psum_pool(name="psum", bufs=4))
         psum_terms = ctx.enter_context(tc.psum_pool(name="psum_terms", bufs=4))
         ctx.enter_context(tc.manual_schedule())
@@ -391,6 +391,8 @@ def tile_napl_conv_withsat_pb_kernel(tc, supports, cheb_2, spatial_attention, x,
                 scalar_group(s)
             if s + 1 < len(FIRST_ROUNDS):
                 products[s + 1] = multiply(s + 1)
+            if s in bank_jobs:
+                fill_banks(*bank_jobs[s])
             if s == final - 1:
                 final_sums = []
                 for i in range(BANK_TILES):
@@ -405,8 +407,6 @@ def tile_napl_conv_withsat_pb_kernel(tc, supports, cheb_2, spatial_attention, x,
             if s == 1:
                 for k in BOTH:
                     interleave_term(psum, k, 0, 1, 0)
-            if s in bank_jobs:
-                fill_banks(*bank_jobs[s])
             for job in turn_jobs.get(s, []):
                 turn_term(*job)
             if s >= 2:

@@ -41,7 +41,7 @@ LAST_ROUNDS = tuple(
 )
 ROUNDS = FIRST_ROUNDS + LAST_ROUNDS
 VECTOR_COLS = (144, 144, 288, 128, 0)
-VECTOR_ATT_COLS = ((512, 256), (0, 128))
+VECTOR_ATT_COLS = ((448, 256), (0, 128))
 
 FLOPS = 2 * TERMS * SAMPLES * NODES * NODES * SIGNAL
 
@@ -357,7 +357,7 @@ def tile_napl_conv_withsat_pb_kernel(tc, supports, cheb_2, spatial_attention, x,
 
         def empty_round(s, engine_copies):
             c, b, ks, u = ROUNDS[s]
-            for i, (k, half, acc) in enumerate(sums[s]):
+            for i, (k, half, acc) in enumerate(sums.get(s, [])):
                 empty_and_store(
                     engine_copies[i % len(engine_copies)], b, k, u * UNIT + half * BANK_COLS, acc[:]
                 )
@@ -381,8 +381,10 @@ def tile_napl_conv_withsat_pb_kernel(tc, supports, cheb_2, spatial_attention, x,
                 regroup_attention(*job)
             for job in turn_jobs.get(s - 1, []):
                 keep_turned_term(*job)
-            groupeds[s] = open_group(s)
             c, b, ks, u = ROUNDS[s]
+            if s == len(FIRST_ROUNDS):
+                quantise_and_contract(s - 1)
+            groupeds[s] = open_group(s)
             if tensor_cols(s):
                 for k in ks:
                     multiply_bank(s, k, 0)
@@ -398,7 +400,7 @@ def tile_napl_conv_withsat_pb_kernel(tc, supports, cheb_2, spatial_attention, x,
                 for i in range(BANK_TILES):
                     final_sums.append(psum_terms.tile([P, BANK_TILES, SIGNAL], F32, name="bank"))
                     add_pass(final_sums[i][:, 0, :], SAMPLES - 1, TERMS - 1, UNITS - 1, 0, BANK_TILES + i)
-            if s >= 1:
+            if s >= 1 and s != len(FIRST_ROUNDS):
                 sums[s - 1] = quantise_and_contract(s - 1)
             if c == LAST:
                 multiply_bank(s, ks[0], 1)

from contextlib import ExitStack

import concourse.masks as masks
import concourse.mybir as mybir

BF16 = mybir.dt.bfloat16
F32 = mybir.dt.float32
U32 = mybir.dt.uint32
U8 = mybir.dt.uint8
FP8X4 = mybir.dt.float8_e4m3fn_x4

P = 128
PACK = 4
SAMPLES = 2
TERMS = 2
NODES = 1024
SIGNAL = 256
PASSES = NODES // (P * PACK)
LAST = PASSES - 1
UNIT = 512
UNITS = NODES // UNIT
M_TILE = 128
BANK_TILES = 2
BANK_COLS = BANK_TILES * M_TILE
BANKS = UNIT // BANK_COLS
RUN = 8
BLOCK = 16
FIRST = (0, 0)
PIECES = ((UNIT, UNIT), (NODES,))
FIRST_ROWS = PACK // 2
BOTH = tuple(range(TERMS))
FIRST_ROUNDS = (
    (0, 0, (0,), 0),
    (0, 0, (1,), 0),
    (0, 1, BOTH, 0),
    (0, 0, BOTH, 1),
    (0, 1, BOTH, 1),
)
LAST_ROUNDS = tuple(
    (LAST, b, (k,), u) for u in range(UNITS) for k in BOTH for b in range(SAMPLES)
)
ROUNDS = FIRST_ROUNDS + LAST_ROUNDS
VECTOR_COLS = (144, 144, 288, 128, 0)
VECTOR_ATT_COLS = ((448, 256), (0, 128))

FLOPS = 2 * TERMS * SAMPLES * NODES * NODES * SIGNAL


def regroup(engine_copy, grouped, rows):
    engine_copy(
        out=grouped.rearrange("p (g i) j -> p g j i", i=RUN),
        in_=rows.rearrange("p j (g i) -> p g j i", i=RUN),
    )


def tensor_width(c, u):
    if c == LAST:
        return UNIT
    return 0 if (c, u) == FIRST else BANK_COLS


def tile_napl_conv_withsat_pb_kernel(tc, supports, cheb_2, spatial_attention, x, out):
    nc = tc.nc
    terms = (supports, cheb_2)
    with ExitStack() as ctx:
        keep = ctx.enter_context(tc.tile_pool(name="keep", bufs=1))
        stage = ctx.enter_context(tc.tile_pool(name="stage", bufs=2))
        stage_first = ctx.enter_context(tc.tile_pool(name="stage_first", bufs=3))
        stage_last = ctx.enter_context(tc.tile_pool(name="stage_last", bufs=2))
        results = ctx.enter_context(tc.tile_pool(name="results", bufs=8))
        psum = ctx.enter_context(tc.psum_pool(name="psum", bufs=4))
        psum_terms = ctx.enter_context(tc.psum_pool(name="psum_terms", bufs=4))
        ctx.enter_context(tc.manual_schedule())

        term_sb = {}
        term_turned = {}
        att_sb = {}
        codes = {}
        scales = {}
        att_grouped = {}
        for c, widths in enumerate(PIECES):
            for i, width in enumerate(widths):
                name = "%d_%d" % (c, i)
                term_sb[c, i] = keep.tile([P, TERMS, PACK, UNIT], BF16, name="term" + name)
                for b in range(SAMPLES):
                    att_sb[b, c, i] = keep.tile([P, PACK, width], BF16, name="att%d_" % b + name)
        term_rows = keep.tile([P, TERMS, PACK, UNIT], BF16)
        for k in range(TERMS):
            term_turned[k] = keep.tile([P, UNIT // P, PACK * P], BF16, name="term_turned%d" % k)
        for s, (c, b, ks, u) in enumerate(ROUNDS):
            width = len(ks) * UNIT
            codes[s] = keep.tile([P, width], U32, name="codes%d" % s, align_bytes=64)
            scales[s] = keep.tile([P, width], U8, name="scales%d" % s, align_bytes=64)
        for b in range(SAMPLES):
            for c in range(PASSES):
                for u in range(UNITS):
                    if (c, u) != FIRST:
                        att_grouped[b, c, u] = keep.tile(
                            [P, tensor_width(c, u), PACK], BF16, name="att_grouped%d_%d_%d" % (b, c, u)
                        )
        x_sb = keep.tile([P, SAMPLES, PASSES, PACK, SIGNAL], BF16)
        x_grouped = keep.tile([P, SAMPLES, PASSES, SIGNAL, PACK], BF16, align_bytes=64)
        x_codes = keep.tile([P, SAMPLES, PASSES, SIGNAL], U32, align_bytes=64)
        x_scales = keep.tile([P, SAMPLES, PASSES, SIGNAL], U8, align_bytes=64)
        diag_bf = keep.tile([P, SAMPLES, PASSES, PACK, BLOCK], BF16)
        diag = keep.tile([P, SAMPLES, PASSES, PACK], F32)
        identity = keep.tile([P, P], BF16)
        masks.make_identity(nc, identity[:])
        identity_f32 = keep.tile([P, P], F32)
        masks.make_identity(nc, identity_f32[:])

        for b in range(SAMPLES):
            flat = spatial_attention[b].rearrange("n m -> (n m)")
            on_diagonal = flat[0 : NODES * NODES : NODES + 1]
            with nc.allow_non_contiguous_dma(reason="a diagonal has no two neighbours"):
                for c in range(PASSES):
                    nc.sync.dma_start(
                        out=diag_bf[:, b, c, :, 0],
                        in_=on_diagonal.rearrange("(c p j) -> c p j", p=P, j=PACK)[c],
                    )
            for c in range(PASSES):
                nc.sync.dma_start(
                    out=x_sb[:, b, c].rearrange("p j s -> p (j s)"),
                    in_=x[b].rearrange("(c p j) f t -> c p (j f t)", p=P, j=PACK)[c],
                )
        def load_rows(slab, matrix, c, cols, first=0, last=PACK):
            rows = matrix[c * P * PACK : (c + 1) * P * PACK, cols]
            nc.sync.dma_start(
                out=slab[:, first:last, :],
                in_=rows.rearrange("(p j) m -> p j m", j=PACK)[:, first:last, :],
            )

        for first in range(0, PACK, FIRST_ROWS):
            for slab, matrix in ((term_sb[0, 0][:, 0], terms[0]), (att_sb[0, 0, 0][:], spatial_attention[0])):
                load_rows(slab, matrix, 0, slice(0, UNIT), first, first + FIRST_ROWS)
        cols = slice(0, UNIT)
        load_rows(term_sb[0, 0][:, 1], terms[1], 0, cols)
        load_rows(att_sb[1, 0, 0][:], spatial_attention[1], 0, cols)
        cols = slice(UNIT, NODES)
        load_rows(att_sb[0, 0, 1][:], spatial_attention[0], 0, cols)
        for k in range(TERMS):
            load_rows(term_sb[0, 1][:, k], terms[k], 0, cols)
        load_rows(att_sb[1, 0, 1][:], spatial_attention[1], 0, cols)
        load_rows(att_sb[0, LAST, 0][:], spatial_attention[0], LAST, slice(0, NODES))
        for k in range(TERMS):
            load_rows(term_sb[LAST, 0][:, k], terms[k], LAST, slice(0, UNIT))
        load_rows(att_sb[1, LAST, 0][:], spatial_attention[1], LAST, slice(0, NODES))
        for k in range(TERMS):
            rows = terms[k][LAST * P * PACK : (LAST + 1) * P * PACK, UNIT:]
            nc.sync.dma_start(out=term_rows[:, k], in_=rows.rearrange("(t p) m -> p t m", p=P))

        def att_cols(b, c, u, first, last):
            piece, base = (u, 0) if c == 0 else (0, u * UNIT)
            return att_sb[b, c, piece][:, :, base + first : base + last]

        for b in range(SAMPLES):
            for c in range(PASSES):
                regroup(nc.vector.tensor_copy, x_grouped[:, b, c], x_sb[:, b, c])
            nc.vector.quantize_mx(
                out=x_codes[:, b].rearrange("p c s -> p (c s)").bitcast(FP8X4),
                scales=x_scales[:, b].rearrange("p c s -> p (c s)"),
                in_=x_grouped[:, b].rearrange("p c s j -> p (c s j)"),
            )

            nc.scalar.copy(out=diag[:, b], in_=diag_bf[:, b, :, :, 0])
            for c in range(PASSES):
                scaled = keep.tile([P, PACK, SIGNAL], F32, name="scaled%d_%d" % (b, c))
                for j in range(PACK):
                    nc.scalar.activation(
                        out=scaled[:, j, :],
                        in_=x_sb[:, b, c, j, :],
                        func=mybir.ActivationFunctionType.Copy,
                        scale=diag[:, b, c, j : j + 1],
                    )
                nc.sync.dma_start(
                    out=out[0, b].rearrange("(c p j) f t -> c p (j f t)", p=P, j=PACK)[c],
                    in_=scaled[:].rearrange("p j s -> p (j s)"),
                )

        def tensor_cols(s):
            c, b, ks, u = ROUNDS[s]
            return tensor_width(c, u)

        def first_copied(s):
            return len(ROUNDS[s][2]) * tensor_cols(s)

        term_grouped = {}

        def interleave_term(pool, k, c, u, half):
            piece = u if c == 0 else 0
            bank = pool.tile([P, BANK_COLS, PACK], BF16, name="bank")
            for i in range(BANK_TILES):
                first = half * BANK_COLS + i * M_TILE
                nc.tensor.matmul(
                    out=bank[:, i * M_TILE : (i + 1) * M_TILE, :].rearrange("p w j -> p j w"),
                    lhsT=identity[:],
                    rhs=term_sb[c, piece][:, k, :, first : first + M_TILE],
                    start=True,
                    stop=True,
                )
            term_grouped[k, c, u, half] = bank

        def turn_term(k, half):
            bank = psum.tile([P, BANK_TILES, PACK * P], BF16, name="bank")
            for i in range(BANK_TILES):
                first = half * BANK_COLS + i * M_TILE
                for t in range(PACK):
                    nc.tensor.transpose(
                        bank[:, i, t * P : (t + 1) * P],
                        term_rows[:, k, t, first : first + M_TILE],
                        identity[:],
                    )
            turned_banks[k, half] = bank

        def keep_turned_term(k, half):
            tiles = slice(half * BANK_TILES, (half + 1) * BANK_TILES)
            nc.scalar.copy(out=term_turned[k][:, tiles, :], in_=turned_banks[k, half][:])

        def turn_term_back(k, half):
            bank = psum_terms.tile([P, BANK_COLS, PACK], BF16, name="bank")
            words = bank[:].bitcast(F32)
            turned = term_turned[k][:].bitcast(F32)
            for i in range(BANK_TILES):
                for r in range(PACK // 2):
                    nc.tensor.transpose(
                        words[:, i * M_TILE : (i + 1) * M_TILE, r],
                        turned[:, half * BANK_TILES + i, r : PACK * P // 2 : 2],
                        identity_f32[:],
                    )
            term_grouped[k, LAST, UNITS - 1, half] = bank

        def fill_banks(k, u):
            for half in range(BANKS):
                if u < UNITS - 1:
                    interleave_term(psum_terms, k, LAST, u, half)
                else:
                    turn_term_back(k, half)

        def regroup_attention(b, c, u):
            width = tensor_width(c, u)
            grouped, rows = att_grouped[b, c, u], att_cols(b, c, u, 0, width)
            split = VECTOR_ATT_COLS[b][u] if c == LAST else 0
            if split:
                regroup(nc.vector.tensor_copy, grouped[:, :split, :], rows[:, :, :split])
            if split < width:
                regroup(nc.scalar.copy, grouped[:, split:, :], rows[:, :, split:])

        def multiply(s):
            c, b, ks, u = ROUNDS[s]
            width = UNIT - tensor_cols(s)
            product = stage.tile([P, PACK, len(ks) * width], BF16, name="product")
            term = term_sb[c, u][:, :, :, tensor_cols(s) :]
            att = att_cols(b, c, u, tensor_cols(s), UNIT)
            if len(ks) == 1:
                rows = FIRST_ROWS if s == 0 else PACK
                for first in range(0, PACK, rows):
                    nc.vector.tensor_tensor(
                        out=product[:, first : first + rows, :],
                        in0=term[:, ks[0], first : first + rows, :],
                        in1=att[:, first : first + rows, :],
                        op=mybir.AluOpType.mult,
                    )
            else:
                nc.vector.tensor_tensor(
                    out=product[:].rearrange("p j (k w) -> p k j w", k=TERMS),
                    in0=term,
                    in1=att.unsqueeze(1).to_broadcast([P, TERMS, PACK, width]),
                    op=mybir.AluOpType.mult,
                )
            return product

        def open_group(s):
            c, b, ks, u = ROUNDS[s]
            pool = stage_first if c == 0 else stage_last
            grouped = pool.tile([P, len(ks) * UNIT, PACK], BF16, align_bytes=64, name="grouped")
            return grouped

        def multiply_bank(s, k, half):
            c, b, ks, u = ROUNDS[s]
            first = ks.index(k) * tensor_cols(s) + half * BANK_COLS
            nc.vector.tensor_tensor(
                out=groupeds[s][:, first : first + BANK_COLS, :],
                in0=term_grouped[k, c, u, half][:],
                in1=att_grouped[b, c, u][:, half * BANK_COLS : (half + 1) * BANK_COLS, :],
                op=mybir.AluOpType.mult,
            )

        def vector_group(s):
            base, split = first_copied(s), VECTOR_COLS[s]
            if split:
                regroup(
                    nc.vector.tensor_copy,
                    groupeds[s][:, base : base + split, :],
                    products[s][:, :, :split],
                )

        def scalar_group(s):
            base, split = first_copied(s), VECTOR_COLS[s]
            if base + split == groupeds[s].shape[1]:
                return
            regroup(nc.scalar.copy, groupeds[s][:, base + split :, :], products[s][:, :, split:])

        def quantise(s, first, last):
            nc.vector.quantize_mx(
                out=codes[s][:, first:last].bitcast(FP8X4),
                scales=scales[s][:, first:last],
                in_=groupeds[s][:, first:last, :].rearrange("p w j -> p (w j)"),
            )

        round_of = {}
        for s, (c, b, ks, u) in enumerate(ROUNDS):
            for k in ks:
                round_of[c, b, k, u] = s

        def code_cols(s, k, i):
            j = ROUNDS[s][2].index(k)
            first = i * M_TILE
            if first < tensor_cols(s):
                first += j * tensor_cols(s)
            else:
                first += first_copied(s) + j * (UNIT - tensor_cols(s)) - tensor_cols(s)
            return slice(first, first + M_TILE)

        def add_pass(sums_of_tile, b, k, u, c, i):
            s = round_of[c, b, k, u]
            cols = code_cols(s, k, i)
            nc.tensor.matmul_mx(
                out=sums_of_tile,
                lhsT=codes[s][:, cols].bitcast(FP8X4),
                lhsT_scale=scales[s][:, cols],
                rhs=x_codes[:, b, c, :].bitcast(FP8X4),
                rhs_scale=x_scales[:, b, c, :],
                start=(c == 0),
                stop=(c == LAST),
            )

        def contract(b, k, u, half):
            acc = psum.tile([P, BANK_TILES, SIGNAL], F32, name="bank")
            for i in range(BANK_TILES):
                for c in range(PASSES):
                    add_pass(acc[:, i, :], b, k, u, c, half * BANK_TILES + i)
            return acc

        def empty_and_store(engine_copy, b, k, first, acc):
            tiles = acc.shape[1]
            result = results.tile([P, tiles, SIGNAL], F32, name="result")
            engine_copy(out=result[:], in_=acc)
            rows = out[1 + k, b, first : first + tiles * M_TILE]
            nc.sync.dma_start(out=rows.rearrange("(t p) f s -> p t (f s)", p=P), in_=result[:])

        def quantise_and_contract(s):
            c, b, ks, u = ROUNDS[s]
            quantise(s, 0, len(ks) * UNIT)
            if c < LAST:
                return []
            return [(k, half, contract(b, k, u, half)) for k in ks for half in range(BANKS)]

        def empty_round(s, engine_copies):
            c, b, ks, u = ROUNDS[s]
            for i, (k, half, acc) in enumerate(sums.get(s, [])):
                empty_and_store(
                    engine_copies[i % len(engine_copies)], b, k, u * UNIT + half * BANK_COLS, acc[:]
                )

        attention_jobs = {2: [(0, 0, 1)], 3: [(1, 0, 1)]}
        late_attention_jobs = {
            4: [(0, LAST, 0), (1, LAST, 0)],
            7: [(0, LAST, 1)],
            8: [(1, LAST, 1)],
        }
        bank_jobs = {3: (0, 0), 4: (1, 0), 7: (0, 1), 9: (1, 1)}
        turn_jobs = {4: [(0, 0), (0, 1)], 5: [(1, 0), (1, 1)]}
        turned_banks = {}

        final = len(ROUNDS) - 1
        products = {0: multiply(0)}
        groupeds = {}
        sums = {}
        for s in range(final):
            for job in attention_jobs.get(s, []):
                regroup_attention(*job)
            for job in turn_jobs.get(s - 1, []):
                keep_turned_term(*job)
            c, b, ks, u = ROUNDS[s]
            if s == len(FIRST_ROUNDS):
                quantise_and_contract(s - 1)
            groupeds[s] = open_group(s)
            if tensor_cols(s):
                for k in ks:
                    multiply_bank(s, k, 0)
            if c == 0:
                vector_group(s)
                scalar_group(s)
            if s + 1 < len(FIRST_ROUNDS):
                products[s + 1] = multiply(s + 1)
            if s in bank_jobs:
                fill_banks(*bank_jobs[s])
            if s == final - 1:
                final_sums = []
                for i in range(BANK_TILES):
                    final_sums.append(psum_terms.tile([P, BANK_TILES, SIGNAL], F32, name="bank"))
                    add_pass(final_sums[i][:, 0, :], SAMPLES - 1, TERMS - 1, UNITS - 1, 0, BANK_TILES + i)
            if s >= 1 and s != len(FIRST_ROUNDS):
                sums[s - 1] = quantise_and_contract(s - 1)
            if c == LAST:
                multiply_bank(s, ks[0], 1)
            for job in late_attention_jobs.get(s, []):
                regroup_attention(*job)
            if s == 1:
                for k in BOTH:
                    interleave_term(psum, k, 0, 1, 0)
            for job in turn_jobs.get(s, []):
                turn_term(*job)
            if s >= 2:
                empty_round(s - 2, (nc.scalar.copy,))

        c, b, ks, u = ROUNDS[final]
        k = ks[0]
        groupeds[final] = open_group(final)
        multiply_bank(final, k, 0)
        sums[final - 1] = quantise_and_contract(final - 1)
        multiply_bank(final, k, 1)
        empty_round(final - 2, (nc.scalar.copy,))
        for half in range(BANKS):
            quantise(final, half * BANK_COLS, (half + 1) * BANK_COLS)
            if half == 0:
                first_sums = contract(b, k, u, half)
            else:
                for i in range(BANK_TILES):
                    add_pass(final_sums[i][:, 0, :], b, k, u, LAST, BANK_TILES + i)
        empty_round(final - 1, (nc.scalar.copy,))
        empty_and_store(nc.vector.tensor_copy, b, k, u * UNIT, first_sums[:])
        for i, engine_copy in enumerate((nc.scalar.copy, nc.vector.tensor_copy)):
            first = u * UNIT + BANK_COLS + i * M_TILE
            empty_and_store(engine_copy, b, k, first, final_sums[i][:, :1, :])
